import numpy as np
import ml_dtypes


def mxq(x, axis, fmt="e4m3"):
    dtype, down = {"e4m3": (ml_dtypes.float8_e4m3fn, 7), "e5m2": (ml_dtypes.float8_e5m2, 14)}[fmt]
    v = np.moveaxis(np.asarray(x, np.float32).astype(ml_dtypes.bfloat16).astype(np.float64), axis, -1)
    blocks = v.reshape(v.shape[:-1] + (-1, 32))
    amax = np.abs(blocks).max(-1, keepdims=True)
    byte = np.maximum(np.where(amax > 0, np.frexp(amax)[1] - 1 + 127, 0) - down, 1)
    scale = np.exp2(byte - 127.0)
    codes = (blocks / scale).astype(np.float32).astype(dtype).astype(np.float64)
    return np.moveaxis((codes * scale).reshape(v.shape), -1, axis)


WIDE = False


def mx_kscale(k):
    if not WIDE:
        return np.ones(k)
    levels = np.array([10, -10, 5, -5, 0])
    a = np.random.permutation(np.resize(levels, k // 512 * 4)).reshape(k // 512, 4)
    idx = np.arange(k)
    return np.exp2(a[idx // 512, idx % 128 // 32])


BF16 = ml_dtypes.bfloat16


def bf(x):
    return np.asarray(x, np.float32).astype(BF16)


def f64(x):
    return np.asarray(x).astype(np.float64)


E2M1 = np.array([0.0, 0.5, 1.0, 1.5, 2.0, 3.0, 4.0, 6.0, -0.0, -0.5, -1.0, -1.5, -2.0, -3.0, -4.0, -6.0])


def pack_weight(w, fmt):
    k, n = w.shape
    w = f64(bf(w)).reshape(k // 32, 32, n)
    amax = np.abs(w).max(1)
    if fmt == "e4m3":
        byte = np.frexp(amax)[1] - 1 + 127 - 7
    else:
        mant, ex = np.frexp(amax / 6.0)
        byte = np.where(mant > 0.5, ex, ex - 1) + 127
    byte = np.clip(np.where(amax > 0, byte, 1), 1, 254)
    scaled = (w * np.exp2(127.0 - byte)[:, None, :]).reshape(k, n).astype(np.float32)
    by_word = np.ascontiguousarray(scaled.reshape(k // 512, 128, 4, n).transpose(0, 1, 3, 2))
    if fmt == "e4m3":
        words = by_word.astype(ml_dtypes.float8_e4m3fn).view(np.uint8)
    else:
        c = by_word.astype(ml_dtypes.float4_e2m1fn).view(np.uint8) & 0xF
        words = c[..., 0::2] | (c[..., 1::2] << 4)
    return np.ascontiguousarray(words), np.ascontiguousarray(byte.astype(np.uint8).reshape(k // 512, 16, n))


def unpack_weight(words, scales, fmt):
    g, p, n, _ = words.shape
    if fmt == "e4m3":
        vals = np.ascontiguousarray(words).view(ml_dtypes.float8_e4m3fn).astype(np.float64)
    else:
        nib = np.empty((g, p, n, 4), np.uint8)
        nib[..., 0::2] = words & 0xF
        nib[..., 1::2] = words >> 4
        vals = E2M1[nib]
    vals = vals * np.repeat(np.exp2(scales.astype(np.float64) - 127.0), 8, axis=1)[..., None]
    return vals.transpose(0, 1, 3, 2).reshape(g * 512, n)

def pack4(w):
    words, scales = pack_weight(w, "e2m1")
    return words.reshape(words.shape[0], 128, -1), scales


def unpack4(words, scales):
    return unpack_weight(words.reshape(words.shape[0], 128, -1, 2), scales, "e2m1")


M, N, E, P, S, B, KT = 1024, 512, 16, 32, 17, 128, 2


def setup_inputs():
    s = mx_kscale(M)
    z = bf(np.random.standard_normal((M, B)) * s[:, None])
    mlp_out = bf(np.random.standard_normal((B, E)) * 0.65)
    t2 = bf(0.5 + 0.1 * np.random.random_sample(1))
    A = bf(np.random.standard_normal((E, M)) * 0.5 / s)
    W = np.random.standard_normal((E, M, M)) / np.sqrt(M) / s
    h = bf(np.random.standard_normal((E, M)) * 0.1)
    cat = np.ascontiguousarray(W.swapaxes(1, 2)).reshape(-1, M)
    W_words, W_scales = pack4(cat)
    return {
        "z": z,
        "mlp_out": mlp_out,
        "t2": t2,
        "A": A,
        "W_words": W_words,
        "W_scales": W_scales,
        "h": h,
    }


def reference(z, mlp_out, t2, A, W_words, W_scales, h):
    z = f64(z)
    lg = -f64(mlp_out).T / f64(t2)[0]
    ex = np.exp(lg - lg.max(axis=0, keepdims=True))
    w_exp = ex / ex.sum(axis=0, keepdims=True)
    zcat = np.concatenate([z[:-P], np.maximum(z[-P:], 0.0)], axis=0)
    Az = f64(A)[:, :, None] * z[None, :, :]
    Wz = unpack4(W_words, W_scales).reshape(E, M, M).swapaxes(1, 2) @ mxq(zcat, 0, "e4m3")
    expert_out = Az + Wz + f64(h)[:, :, None]
    return np.sum(expert_out * w_exp[:, None, :], axis=0)

@@ -1,0 +1,207 @@
+from contextlib import ExitStack
+
+import concourse.mybir as mybir
+from concourse.masks import make_identity
+
+F32 = mybir.dt.float32
+BF16 = mybir.dt.bfloat16
+I32 = mybir.dt.int32
+U32 = mybir.dt.uint32
+U8 = mybir.dt.uint8
+FP8X4 = mybir.dt.float8_e4m3fn_x4
+FP4X4 = mybir.dt.float4_e2m1fn_x4
+ALU = mybir.AluOpType
+ACT = mybir.ActivationFunctionType
+AX = mybir.AxisListType
+
+P = 128
+PACK = 4
+K_PASS = P * PACK
+M = 1024
+B = 128
+E = 16
+RELU_ROWS = 32
+PASSES = M // K_PASS
+N_TILE = 512
+HALVES = M // N_TILE
+M_TILES = N_TILE // P
+QUADRANT = 32
+
+GROUP_EXPERTS = 4
+GROUPS = E // GROUP_EXPERTS
+GROUP_PASSES = GROUP_EXPERTS * PASSES
+
+FLOPS = 2 * E * M * M * B
+
+
+def tile_dynamix_pb_e_kernel(tc, z, mlp_out, t2, A, W_words, W_scales, h, out):
+    nc = tc.nc
+    with ExitStack() as ctx:
+        keep = ctx.enter_context(tc.tile_pool(name="keep", bufs=1))
+        stage = ctx.enter_context(tc.tile_pool(name="stage", bufs=2))
+        psum = ctx.enter_context(tc.psum_pool(name="psum", bufs=8))
+        ctx.enter_context(tc.manual_schedule())
+
+        words = keep.tile([P, E * PASSES, 2 * M], U8, align_bytes=64)
+        planes = keep.tile([P, E * PASSES, M], U8, align_bytes=64)
+        words_i32 = words[:].bitcast(I32)
+        planes_i32 = planes[:].bitcast(I32)
+        w_words_i32 = W_words.bitcast(I32)
+        w_scales_i32 = W_scales.bitcast(I32)
+
+        def zero_planes(group):
+            passes = slice(group * GROUP_PASSES, (group + 1) * GROUP_PASSES)
+            nc.vector.memset(planes_i32[:, passes, :], 0)
+
+        def load_scales(group):
+            passes = slice(group * GROUP_PASSES, (group + 1) * GROUP_PASSES)
+            for s in range(2):
+                for r in range(PACK):
+                    nc.sync.dma_start(
+                        out=planes_i32[QUADRANT * s + r : P : 2 * QUADRANT, passes, :],
+                        in_=w_scales_i32[passes, PACK * s + r : 16 : 8, :].rearrange("g q n -> q g n"),
+                    )
+
+        def load_words(group):
+            for g in range(group * GROUP_PASSES, (group + 1) * GROUP_PASSES):
+                nc.sync.dma_start(out=words_i32[:, g, :], in_=w_words_i32[g])
+
+        z_k = keep.tile([P, PASSES, PACK, B], BF16)
+        nc.sync.dma_start(
+            out=z_k[:].rearrange("p g j b -> p g (j b)"),
+            in_=z.rearrange("(g p j) b -> p g (j b)", g=PASSES, p=P, j=PACK),
+        )
+        logits = keep.tile([P, E], BF16)
+        nc.scalar.dma_start(out=logits[:], in_=mlp_out)
+        t2_all = keep.tile([P, 1], BF16)
+        nc.scalar.dma_start(out=t2_all[:], in_=t2.partition_broadcast(P))
+        a_bf = keep.tile([E, M], BF16)
+        nc.scalar.dma_start(out=a_bf[:], in_=A)
+        h_bf = keep.tile([E, M], BF16)
+        nc.scalar.dma_start(out=h_bf[:], in_=h)
+
+        for group in range(GROUPS // 2):
+            zero_planes(group)
+        for group in range(GROUPS // 2):
+            load_scales(group)
+            load_words(group)
+
+        warm_in = keep.tile([P, 1], F32)
+        warm_out = keep.tile([P, 1], F32)
+        nc.gpsimd.memset(warm_in[:], 0.0)
+        nc.scalar.activation(out=warm_out[:], in_=warm_in[:], func=ACT.Exp)
+        ident_f32 = keep.tile([P, P], F32)
+        make_identity(nc, ident_f32[:])
+        ex_pad = keep.tile([P, P], F32)
+        nc.gpsimd.memset(ex_pad[:], 0.0)
+        ah32 = keep.tile([P, 2, M], F32)
+        nc.gpsimd.memset(ah32[:], 0.0)
+        ident_bf = keep.tile([P, P], BF16)
+        make_identity(nc, ident_bf[:])
+
+        inv_t = keep.tile([P, 1], F32)
+        nc.vector.reciprocal(out=inv_t[:], in_=t2_all[:])
+        u = keep.tile([P, E], F32)
+        nc.vector.tensor_scalar(out=u[:], in0=logits[:], scalar1=inv_t[:], scalar2=None, op0=ALU.mult)
+        u_min = keep.tile([P, 1], F32)
+        nc.vector.tensor_reduce(out=u_min[:], in_=u[:], axis=AX.X, op=ALU.min)
+        ex_sum = keep.tile([P, 1], F32)
+        nc.scalar.activation(
+            out=ex_pad[:, 0:E], in_=u[:], func=ACT.Exp, bias=u_min[:], scale=-1.0, accum_out=ex_sum[:]
+        )
+        nc.scalar.copy(out=ah32[0:E, 0, :], in_=a_bf[:])
+
+        relu_parts = keep.tile([P, 1], F32)
+        nc.vector.reduce_sum(out=relu_parts[:], in_=ident_f32[:, P - RELU_ROWS // PACK : P], axis=AX.X)
+        rows_kept = keep.tile([P, PASSES], F32)
+        nc.vector.memset(rows_kept[:], 1.0)
+        nc.vector.tensor_scalar(
+            out=rows_kept[:, PASSES - 1 : PASSES], in0=relu_parts[:], scalar1=-1.0, scalar2=1.0, op0=ALU.mult, op1=ALU.add
+        )
+        grouped = keep.tile([P, PASSES, B, PACK], BF16, align_bytes=64)
+        for g in range(PASSES):
+            z_bj = z_k[:, g].rearrange("p j b -> p b j")
+            nc.vector.scalar_tensor_tensor(
+                out=grouped[:, g], in0=z_bj, scalar=rows_kept[:, g : g + 1], in1=z_bj, op0=ALU.mult, op1=ALU.max
+            )
+        zq = keep.tile([P, PASSES * B], U32, align_bytes=64)
+        zq_scales = keep.tile([P, PASSES * B], U8, align_bytes=64)
+        for group in range(GROUPS // 2, GROUPS):
+            zero_planes(group)
+        for group in range(GROUPS // 2, GROUPS):
+            load_scales(group)
+            load_words(group)
+        inv_sum = keep.tile([P, 1], F32)
+        nc.vector.reciprocal(out=inv_sum[:], in_=ex_sum[:])
+        gate = keep.tile([P, E], F32)
+        nc.vector.tensor_scalar(out=gate[:], in0=ex_pad[:, 0:E], scalar1=inv_sum[:], scalar2=None, op0=ALU.mult)
+        nc.vector.quantize_mx(
+            out=zq[:].bitcast(FP8X4), scales=zq_scales[:], in_=grouped[:].rearrange("p g b j -> p (g b j)")
+        )
+
+        zT_ps = psum.tile([P, PASSES, PACK, P], BF16, tag="bank")
+        for g in range(PASSES):
+            for j in range(PACK):
+                nc.tensor.transpose(out=zT_ps[:, g, j, :], in_=z_k[:, g, j, :], identity=ident_bf[:])
+        exT_ps = psum.tile([P, P], F32, tag="bank")
+        nc.tensor.transpose(out=exT_ps[:], in_=ex_pad[:], identity=ident_f32[:])
+        exT = keep.tile([P, P], F32)
+        nc.scalar.copy(out=exT[:], in_=exT_ps[:])
+        nc.scalar.copy(out=ah32[0:E, 1, :], in_=h_bf[:])
+        zT = keep.tile([P, PASSES, P, PACK], BF16)
+        nc.scalar.copy(out=zT[:], in_=zT_ps[:].rearrange("b g j p -> b g p j"))
+        zT_m = zT[:].rearrange("b g p j -> b (g p j)")
+
+        acc = keep.tile([P, M], F32)
+        az = keep.tile([P, M], F32)
+        mixed = {}
+        for term in range(2):
+            for half in range(HALVES):
+                cols = slice(half * N_TILE, (half + 1) * N_TILE)
+                mixed[term, half] = psum.tile([P, N_TILE], F32, tag="bank", name="mixed")
+                nc.tensor.matmul(out=mixed[term, half][:], lhsT=exT[:], rhs=ah32[:, term, cols], start=True, stop=True)
+        for half in range(HALVES):
+            cols = slice(half * N_TILE, (half + 1) * N_TILE)
+            nc.vector.scalar_tensor_tensor(
+                out=az[:, cols], in0=mixed[0, half][:], scalar=inv_sum[:], in1=zT_m[:, cols], op0=ALU.mult, op1=ALU.mult
+            )
+        for half in range(HALVES):
+            cols = slice(half * N_TILE, (half + 1) * N_TILE)
+            nc.vector.scalar_tensor_tensor(
+                out=acc[:, cols], in0=mixed[1, half][:], scalar=inv_sum[:], in1=az[:, cols], op0=ALU.mult, op1=ALU.add
+            )
+
+        for e in range(E):
+            y = {}
+            for half in range(HALVES):
+                y[half] = psum.tile([P, N_TILE], F32, tag="bank", name="y")
+            for c in range(PASSES):
+                g = e * PASSES + c
+                for half in range(HALVES):
+                    nc.tensor.matmul_mx(
+                        out=y[half][:],
+                        lhsT=zq[:, c * B : (c + 1) * B].bitcast(FP8X4),
+                        lhsT_scale=zq_scales[:, c * B : (c + 1) * B],
+                        rhs=words[:, g, half * 2 * N_TILE : (half + 1) * 2 * N_TILE].bitcast(FP4X4),
+                        rhs_scale=planes[:, g, half * N_TILE : (half + 1) * N_TILE],
+                        start=(c == 0),
+                        stop=(c == PASSES - 1),
+                    )
+            for half in range(HALVES):
+                cols = slice(half * N_TILE, (half + 1) * N_TILE)
+                nc.vector.scalar_tensor_tensor(
+                    out=acc[:, cols], in0=y[half][:], scalar=gate[:, e : e + 1], in1=acc[:, cols], op0=ALU.mult, op1=ALU.add
+                )
+
+        out_pib = out.rearrange("(i p) b -> p i b", p=P)
+        for half in range(HALVES):
+            accT = psum.tile([P, M_TILES, B], F32, tag="bank")
+            for i in range(M_TILES):
+                first = (half * M_TILES + i) * P
+                nc.tensor.transpose(out=accT[:, i, :], in_=acc[:, first : first + P], identity=ident_f32[:])
+            result = stage.tile([P, M_TILES, B], F32)
+            if half % 2 == 0:
+                nc.scalar.copy(out=result[:], in_=accT[:])
+            else:
+                nc.vector.tensor_copy(out=result[:], in_=accT[:])
+            nc.sync.dma_start(out=out_pib[:, half * M_TILES : (half + 1) * M_TILES, :], in_=result[:])

@@ -43,22 +43,20 @@ def tile_dynamix_pb_e_kernel(tc, z, mlp_out, t2, A, W_words, W_scales, h, out):
         ctx.enter_context(tc.manual_schedule())
 
         words = keep.tile([P, E * PASSES, 2 * M], U8, align_bytes=64)
-        planes = keep.tile([P, E * PASSES, M], U8, align_bytes=64)
+        planes = [keep.tile([P, GROUP_PASSES, M], U8, align_bytes=64, name="planes%d" % group) for group in range(GROUPS)]
         words_i32 = words[:].bitcast(I32)
-        planes_i32 = planes[:].bitcast(I32)
         w_words_i32 = W_words.bitcast(I32)
         w_scales_i32 = W_scales.bitcast(I32)
 
         def zero_planes(group):
-            passes = slice(group * GROUP_PASSES, (group + 1) * GROUP_PASSES)
-            nc.vector.memset(planes_i32[:, passes, :], 0)
+            nc.vector.memset(planes[group][:].bitcast(I32), 0)
 
         def load_scales(group):
             passes = slice(group * GROUP_PASSES, (group + 1) * GROUP_PASSES)
             for s in range(2):
                 for r in range(PACK):
                     nc.sync.dma_start(
-                        out=planes_i32[QUADRANT * s + r : P : 2 * QUADRANT, passes, :],
+                        out=planes[group][:].bitcast(I32)[QUADRANT * s + r : P : 2 * QUADRANT, :, :],
                         in_=w_scales_i32[passes, PACK * s + r : 16 : 8, :].rearrange("g q n -> q g n"),
                     )
 
@@ -183,7 +181,7 @@ def tile_dynamix_pb_e_kernel(tc, z, mlp_out, t2, A, W_words, W_scales, h, out):
                         lhsT=zq[:, c * B : (c + 1) * B].bitcast(FP8X4),
                         lhsT_scale=zq_scales[:, c * B : (c + 1) * B],
                         rhs=words[:, g, half * 2 * N_TILE : (half + 1) * 2 * N_TILE].bitcast(FP4X4),
-                        rhs_scale=planes[:, g, half * N_TILE : (half + 1) * N_TILE],
+                        rhs_scale=planes[e // GROUP_EXPERTS][:, g % GROUP_PASSES, half * N_TILE : (half + 1) * N_TILE],
                         start=(c == 0),
                         stop=(c == PASSES - 1),
                     )

@@ -27,7 +27,7 @@ HALVES = M // N_TILE
 M_TILES = N_TILE // P
 QUADRANT = 32
 
-GROUP_EXPERTS = 4
+GROUP_EXPERTS = 8
 GROUPS = E // GROUP_EXPERTS
 GROUP_PASSES = GROUP_EXPERTS * PASSES
 
@@ -53,15 +53,17 @@ def tile_dynamix_pb_e_kernel(tc, z, mlp_out, t2, A, W_words, W_scales, h, out):
 
         def load_scales(group):
             passes = slice(group * GROUP_PASSES, (group + 1) * GROUP_PASSES)
-            for s in range(2):
-                for r in range(PACK):
+            for r in range(PACK):
+                for quadrant in (0, 2, 1, 3):
+                    q = PACK * quadrant + r
+                    row = QUADRANT * quadrant + r
                     nc.sync.dma_start(
-                        out=planes[group][:].bitcast(I32)[QUADRANT * s + r : P : 2 * QUADRANT, :, :],
-                        in_=w_scales_i32[passes, PACK * s + r : 16 : 8, :].rearrange("g q n -> q g n"),
+                        out=planes[group][:].bitcast(I32)[row : row + 1, :, :],
+                        in_=w_scales_i32[passes, q : q + 1, :].rearrange("g q n -> q g n"),
                     )
 
-        def load_words(group):
-            for g in range(group * GROUP_PASSES, (group + 1) * GROUP_PASSES):
+        def load_words(first_expert, last_expert):
+            for g in range(first_expert * PASSES, (last_expert + 1) * PASSES):
                 nc.sync.dma_start(out=words_i32[:, g, :], in_=w_words_i32[g])
 
         z_k = keep.tile([P, PASSES, PACK, B], BF16)
@@ -78,11 +80,10 @@ def tile_dynamix_pb_e_kernel(tc, z, mlp_out, t2, A, W_words, W_scales, h, out):
         h_bf = keep.tile([E, M], BF16)
         nc.scalar.dma_start(out=h_bf[:], in_=h)
 
-        for group in range(GROUPS // 2):
-            zero_planes(group)
-        for group in range(GROUPS // 2):
-            load_scales(group)
-            load_words(group)
+        zero_planes(0)
+        load_words(0, 0)
+        load_scales(0)
+        load_words(1, GROUP_EXPERTS - 1)
 
         warm_in = keep.tile([P, 1], F32)
         warm_out = keep.tile([P, 1], F32)
@@ -124,11 +125,10 @@ def tile_dynamix_pb_e_kernel(tc, z, mlp_out, t2, A, W_words, W_scales, h, out):
             )
         zq = keep.tile([P, PASSES * B], U32, align_bytes=64)
         zq_scales = keep.tile([P, PASSES * B], U8, align_bytes=64)
-        for group in range(GROUPS // 2, GROUPS):
+        for group in range(1, GROUPS):
             zero_planes(group)
-        for group in range(GROUPS // 2, GROUPS):
             load_scales(group)
-            load_words(group)
+            load_words(group * GROUP_EXPERTS, (group + 1) * GROUP_EXPERTS - 1)
         inv_sum = keep.tile([P, 1], F32)
         nc.vector.reciprocal(out=inv_sum[:], in_=ex_sum[:])
         gate = keep.tile([P, E], F32)

@@ -27,9 +27,10 @@ HALVES = M // N_TILE
 M_TILES = N_TILE // P
 QUADRANT = 32
 
-GROUP_EXPERTS = 8
-GROUPS = E // GROUP_EXPERTS
-GROUP_PASSES = GROUP_EXPERTS * PASSES
+FIRST_EXPERTS = 4
+LAST_EXPERTS = 4
+PARTS = 3
+COPIES = P // E
 
 FLOPS = 2 * E * M * M * B
 
@@ -43,28 +44,32 @@ def tile_dynamix_pb_e_kernel(tc, z, mlp_out, t2, A, W_words, W_scales, h, out):
         ctx.enter_context(tc.manual_schedule())
 
         words = keep.tile([P, E * PASSES, 2 * M], U8, align_bytes=64)
-        planes = [keep.tile([P, GROUP_PASSES, M], U8, align_bytes=64, name="planes%d" % group) for group in range(GROUPS)]
         words_i32 = words[:].bitcast(I32)
         w_words_i32 = W_words.bitcast(I32)
-        w_scales_i32 = W_scales.bitcast(I32)
+        first_passes = FIRST_EXPERTS * PASSES
+        planes_first = keep.tile([P, first_passes, M], U8, align_bytes=64)
+        planes_rest = keep.tile([P, E * PASSES - first_passes, M], U8, align_bytes=64)
 
-        def zero_planes(group):
-            nc.vector.memset(planes[group][:].bitcast(I32), 0)
-
-        def load_scales(group):
-            passes = slice(group * GROUP_PASSES, (group + 1) * GROUP_PASSES)
-            for r in range(PACK):
-                for quadrant in (0, 2, 1, 3):
-                    q = PACK * quadrant + r
-                    row = QUADRANT * quadrant + r
-                    nc.sync.dma_start(
-                        out=planes[group][:].bitcast(I32)[row : row + 1, :, :],
-                        in_=w_scales_i32[passes, q : q + 1, :].rearrange("g q n -> q g n"),
+        def load_scales(queue, view, planes, passes, quadrants_apart):
+            for s in range(quadrants_apart):
+                for r in range(PACK):
+                    queue.dma_start(
+                        out=planes[:].bitcast(view)[QUADRANT * s + r : P : QUADRANT * quadrants_apart, :, :],
+                        in_=W_scales.bitcast(view)[passes, PACK * s + r : 16 : PACK * quadrants_apart, :].rearrange(
+                            "g q n -> q g n"
+                        ),
                     )
 
-        def load_words(first_expert, last_expert):
-            for g in range(first_expert * PASSES, (last_expert + 1) * PASSES):
+        def load_words(first_expert, end_expert):
+            for g in range(first_expert * PASSES, end_expert * PASSES):
                 nc.sync.dma_start(out=words_i32[:, g, :], in_=w_words_i32[g])
+
+        warm_in = keep.tile([P, 1], F32)
+        warm_out = keep.tile([P, 1], F32)
+        nc.gpsimd.memset(warm_in[:], 0.0)
+        nc.scalar.activation(out=warm_out[:], in_=warm_in[:], func=ACT.Exp)
+        nc.gpsimd.memset(planes_first[:].bitcast(F32), 0.0)
+        nc.vector.memset(planes_rest[:].bitcast(I32), 0)
 
         z_k = keep.tile([P, PASSES, PACK, B], BF16)
         nc.sync.dma_start(
@@ -75,28 +80,20 @@ def tile_dynamix_pb_e_kernel(tc, z, mlp_out, t2, A, W_words, W_scales, h, out):
         nc.scalar.dma_start(out=logits[:], in_=mlp_out)
         t2_all = keep.tile([P, 1], BF16)
         nc.scalar.dma_start(out=t2_all[:], in_=t2.partition_broadcast(P))
-        a_bf = keep.tile([E, M], BF16)
-        nc.scalar.dma_start(out=a_bf[:], in_=A)
-        h_bf = keep.tile([E, M], BF16)
-        nc.scalar.dma_start(out=h_bf[:], in_=h)
+        load_scales(nc.sync, I32, planes_first, slice(0, first_passes), 2)
+        load_words(0, 2)
+        ah = keep.tile([P, 2, M], BF16)
+        nc.sync.dma_start(out=ah[:, 0, :], in_=A.unsqueeze(1).to_broadcast([E, COPIES, M]))
+        nc.sync.dma_start(out=ah[:, 1, :], in_=h.unsqueeze(1).to_broadcast([E, COPIES, M]))
+        load_words(2, E)
 
-        zero_planes(0)
-        load_words(0, 0)
-        load_scales(0)
-        load_words(1, GROUP_EXPERTS - 1)
-
-        warm_in = keep.tile([P, 1], F32)
-        warm_out = keep.tile([P, 1], F32)
-        nc.gpsimd.memset(warm_in[:], 0.0)
-        nc.scalar.activation(out=warm_out[:], in_=warm_in[:], func=ACT.Exp)
         ident_f32 = keep.tile([P, P], F32)
         make_identity(nc, ident_f32[:])
-        ex_pad = keep.tile([P, P], F32)
-        nc.gpsimd.memset(ex_pad[:], 0.0)
-        ah32 = keep.tile([P, 2, M], F32)
-        nc.gpsimd.memset(ah32[:], 0.0)
         ident_bf = keep.tile([P, P], BF16)
         make_identity(nc, ident_bf[:])
+        ex_parts = keep.tile([P, E, COPIES], BF16)
+        nc.gpsimd.memset(ex_parts[:], 0.0)
+        load_scales(nc.gpsimd, F32, planes_rest, slice(first_passes, E * PASSES), 1)
 
         inv_t = keep.tile([P, 1], F32)
         nc.vector.reciprocal(out=inv_t[:], in_=t2_all[:])
@@ -104,11 +101,9 @@ def tile_dynamix_pb_e_kernel(tc, z, mlp_out, t2, A, W_words, W_scales, h, out):
         nc.vector.tensor_scalar(out=u[:], in0=logits[:], scalar1=inv_t[:], scalar2=None, op0=ALU.mult)
         u_min = keep.tile([P, 1], F32)
         nc.vector.tensor_reduce(out=u_min[:], in_=u[:], axis=AX.X, op=ALU.min)
+        ex = keep.tile([P, E], F32)
         ex_sum = keep.tile([P, 1], F32)
-        nc.scalar.activation(
-            out=ex_pad[:, 0:E], in_=u[:], func=ACT.Exp, bias=u_min[:], scale=-1.0, accum_out=ex_sum[:]
-        )
-        nc.scalar.copy(out=ah32[0:E, 0, :], in_=a_bf[:])
+        nc.scalar.activation(out=ex[:], in_=u[:], func=ACT.Exp, bias=u_min[:], scale=-1.0, accum_out=ex_sum[:])
 
         relu_parts = keep.tile([P, 1], F32)
         nc.vector.reduce_sum(out=relu_parts[:], in_=ident_f32[:, P - RELU_ROWS // PACK : P], axis=AX.X)
@@ -125,71 +120,81 @@ def tile_dynamix_pb_e_kernel(tc, z, mlp_out, t2, A, W_words, W_scales, h, out):
             )
         zq = keep.tile([P, PASSES * B], U32, align_bytes=64)
         zq_scales = keep.tile([P, PASSES * B], U8, align_bytes=64)
-        for group in range(1, GROUPS):
-            zero_planes(group)
-            load_scales(group)
-            load_words(group * GROUP_EXPERTS, (group + 1) * GROUP_EXPERTS - 1)
         inv_sum = keep.tile([P, 1], F32)
         nc.vector.reciprocal(out=inv_sum[:], in_=ex_sum[:])
         gate = keep.tile([P, E], F32)
-        nc.vector.tensor_scalar(out=gate[:], in0=ex_pad[:, 0:E], scalar1=inv_sum[:], scalar2=None, op0=ALU.mult)
+        nc.vector.tensor_scalar(out=gate[:], in0=ex[:], scalar1=inv_sum[:], scalar2=None, op0=ALU.mult)
         nc.vector.quantize_mx(
             out=zq[:].bitcast(FP8X4), scales=zq_scales[:], in_=grouped[:].rearrange("p g b j -> p (g b j)")
         )
+        left = ex
+        for part in range(PARTS):
+            nc.vector.tensor_copy(out=ex_parts[:, :, part], in_=left[:])
+            if part < PARTS - 1:
+                still_left = keep.tile([P, E], F32, name="left%d" % part)
+                nc.vector.tensor_tensor(out=still_left[:], in0=left[:], in1=ex_parts[:, :, part], op=ALU.subtract)
+                left = still_left
 
         zT_ps = psum.tile([P, PASSES, PACK, P], BF16, tag="bank")
         for g in range(PASSES):
             for j in range(PACK):
                 nc.tensor.transpose(out=zT_ps[:, g, j, :], in_=z_k[:, g, j, :], identity=ident_bf[:])
-        exT_ps = psum.tile([P, P], F32, tag="bank")
-        nc.tensor.transpose(out=exT_ps[:], in_=ex_pad[:], identity=ident_f32[:])
-        exT = keep.tile([P, P], F32)
-        nc.scalar.copy(out=exT[:], in_=exT_ps[:])
-        nc.scalar.copy(out=ah32[0:E, 1, :], in_=h_bf[:])
         zT = keep.tile([P, PASSES, P, PACK], BF16)
         nc.scalar.copy(out=zT[:], in_=zT_ps[:].rearrange("b g j p -> b g p j"))
-        zT_m = zT[:].rearrange("b g p j -> b (g p j)")
+        exT_ps = psum.tile([P, P], BF16, tag="bank")
+        nc.tensor.transpose(out=exT_ps[:], in_=ex_parts[:].rearrange("b e i -> b (e i)"), identity=ident_bf[:])
+        exT = keep.tile([P, P], BF16)
+        nc.scalar.copy(out=exT[:], in_=exT_ps[:])
 
         acc = keep.tile([P, M], F32)
-        az = keep.tile([P, M], F32)
-        mixed = {}
+
+        def experts(first_expert, end_expert):
+            for e in range(first_expert, end_expert):
+                y = {}
+                for half in range(HALVES):
+                    y[half] = psum.tile([P, N_TILE], F32, tag="bank", name="y")
+                for c in range(PASSES):
+                    g = e * PASSES + c
+                    plane = planes_first[:, g, :] if e < FIRST_EXPERTS else planes_rest[:, g - first_passes, :]
+                    for half in range(HALVES):
+                        nc.tensor.matmul_mx(
+                            out=y[half][:],
+                            lhsT=zq[:, c * B : (c + 1) * B].bitcast(FP8X4),
+                            lhsT_scale=zq_scales[:, c * B : (c + 1) * B],
+                            rhs=words[:, g, half * 2 * N_TILE : (half + 1) * 2 * N_TILE].bitcast(FP4X4),
+                            rhs_scale=plane[:, half * N_TILE : (half + 1) * N_TILE],
+                            start=(c == 0),
+                            stop=(c == PASSES - 1),
+                        )
+                for half in range(HALVES):
+                    cols = slice(half * N_TILE, (half + 1) * N_TILE)
+                    if e == 0:
+                        nc.vector.tensor_scalar(
+                            out=acc[:, cols], in0=y[half][:], scalar1=gate[:, e : e + 1], scalar2=None, op0=ALU.mult
+                        )
+                    else:
+                        nc.vector.scalar_tensor_tensor(
+                            out=acc[:, cols], in0=y[half][:], scalar=gate[:, e : e + 1], in1=acc[:, cols],
+                            op0=ALU.mult, op1=ALU.add,
+                        )
+
+        experts(0, FIRST_EXPERTS)
+
+        gate_a = keep.tile([P, M], F32)
+        side = keep.tile([P, M], F32)
+        mixed_sb = (gate_a, side)
         for term in range(2):
             for half in range(HALVES):
                 cols = slice(half * N_TILE, (half + 1) * N_TILE)
-                mixed[term, half] = psum.tile([P, N_TILE], F32, tag="bank", name="mixed")
-                nc.tensor.matmul(out=mixed[term, half][:], lhsT=exT[:], rhs=ah32[:, term, cols], start=True, stop=True)
-        for half in range(HALVES):
-            cols = slice(half * N_TILE, (half + 1) * N_TILE)
-            nc.vector.scalar_tensor_tensor(
-                out=az[:, cols], in0=mixed[0, half][:], scalar=inv_sum[:], in1=zT_m[:, cols], op0=ALU.mult, op1=ALU.mult
-            )
-        for half in range(HALVES):
-            cols = slice(half * N_TILE, (half + 1) * N_TILE)
-            nc.vector.scalar_tensor_tensor(
-                out=acc[:, cols], in0=mixed[1, half][:], scalar=inv_sum[:], in1=az[:, cols], op0=ALU.mult, op1=ALU.add
-            )
+                mixed = psum.tile([P, N_TILE], F32, tag="bank")
+                nc.tensor.matmul(out=mixed[:], lhsT=exT[:], rhs=ah[:, term, cols], start=True, stop=True)
+                nc.scalar.activation(out=mixed_sb[term][:, cols], in_=mixed[:], func=ACT.Copy, scale=inv_sum[:])
+        nc.gpsimd.tensor_tensor(out=gate_a[:], in0=gate_a[:], in1=zT[:].rearrange("b g p j -> b (g p j)"), op=ALU.mult)
+        nc.gpsimd.tensor_tensor(out=side[:], in0=side[:], in1=gate_a[:], op=ALU.add)
 
-        for e in range(E):
-            y = {}
-            for half in range(HALVES):
-                y[half] = psum.tile([P, N_TILE], F32, tag="bank", name="y")
-            for c in range(PASSES):
-                g = e * PASSES + c
-                for half in range(HALVES):
-                    nc.tensor.matmul_mx(
-                        out=y[half][:],
-                        lhsT=zq[:, c * B : (c + 1) * B].bitcast(FP8X4),
-                        lhsT_scale=zq_scales[:, c * B : (c + 1) * B],
-                        rhs=words[:, g, half * 2 * N_TILE : (half + 1) * 2 * N_TILE].bitcast(FP4X4),
-                        rhs_scale=planes[e // GROUP_EXPERTS][:, g % GROUP_PASSES, half * N_TILE : (half + 1) * N_TILE],
-                        start=(c == 0),
-                        stop=(c == PASSES - 1),
-                    )
-            for half in range(HALVES):
-                cols = slice(half * N_TILE, (half + 1) * N_TILE)
-                nc.vector.scalar_tensor_tensor(
-                    out=acc[:, cols], in0=y[half][:], scalar=gate[:, e : e + 1], in1=acc[:, cols], op0=ALU.mult, op1=ALU.add
-                )
+        experts(FIRST_EXPERTS, E - LAST_EXPERTS)
+        nc.vector.tensor_tensor(out=acc[:], in0=acc[:], in1=side[:], op=ALU.add)
+        experts(E - LAST_EXPERTS, E)
 
         out_pib = out.rearrange("(i p) b -> p i b", p=P)
         for half in range(HALVES):

@@ -27,10 +27,10 @@ HALVES = M // N_TILE
 M_TILES = N_TILE // P
 QUADRANT = 32
 
-FIRST_EXPERTS = 4
-LAST_EXPERTS = 4
-PARTS = 3
-COPIES = P // E
+GROUP_EXPERTS = 4
+GROUPS = E // GROUP_EXPERTS
+GROUP_PASSES = GROUP_EXPERTS * PASSES
+SCALE_DMA_PASSES = 4
 
 FLOPS = 2 * E * M * M * B
 
@@ -44,32 +44,28 @@ def tile_dynamix_pb_e_kernel(tc, z, mlp_out, t2, A, W_words, W_scales, h, out):
         ctx.enter_context(tc.manual_schedule())
 
         words = keep.tile([P, E * PASSES, 2 * M], U8, align_bytes=64)
+        planes = [keep.tile([P, GROUP_PASSES, M], U8, align_bytes=64, name="planes%d" % group) for group in range(GROUPS)]
         words_i32 = words[:].bitcast(I32)
         w_words_i32 = W_words.bitcast(I32)
-        first_passes = FIRST_EXPERTS * PASSES
-        planes_first = keep.tile([P, first_passes, M], U8, align_bytes=64)
-        planes_rest = keep.tile([P, E * PASSES - first_passes, M], U8, align_bytes=64)
+        w_scales_i32 = W_scales.bitcast(I32)
 
-        def load_scales(queue, view, planes, passes, quadrants_apart):
-            for s in range(quadrants_apart):
-                for r in range(PACK):
-                    queue.dma_start(
-                        out=planes[:].bitcast(view)[QUADRANT * s + r : P : QUADRANT * quadrants_apart, :, :],
-                        in_=W_scales.bitcast(view)[passes, PACK * s + r : 16 : PACK * quadrants_apart, :].rearrange(
-                            "g q n -> q g n"
-                        ),
-                    )
+        def zero_planes(group):
+            nc.vector.memset(planes[group][:].bitcast(I32), 0)
 
-        def load_words(first_expert, end_expert):
-            for g in range(first_expert * PASSES, end_expert * PASSES):
+        def load_scales(group):
+            for first in range(0, GROUP_PASSES, SCALE_DMA_PASSES):
+                local = slice(first, first + SCALE_DMA_PASSES)
+                passes = slice(group * GROUP_PASSES + first, group * GROUP_PASSES + first + SCALE_DMA_PASSES)
+                for s in range(2):
+                    for r in range(PACK):
+                        nc.sync.dma_start(
+                            out=planes[group][:].bitcast(I32)[QUADRANT * s + r : P : 2 * QUADRANT, local, :],
+                            in_=w_scales_i32[passes, PACK * s + r : 16 : 8, :].rearrange("g q n -> q g n"),
+                        )
+
+        def load_words(group):
+            for g in range(group * GROUP_PASSES, (group + 1) * GROUP_PASSES):
                 nc.sync.dma_start(out=words_i32[:, g, :], in_=w_words_i32[g])
-
-        warm_in = keep.tile([P, 1], F32)
-        warm_out = keep.tile([P, 1], F32)
-        nc.gpsimd.memset(warm_in[:], 0.0)
-        nc.scalar.activation(out=warm_out[:], in_=warm_in[:], func=ACT.Exp)
-        nc.gpsimd.memset(planes_first[:].bitcast(F32), 0.0)
-        nc.vector.memset(planes_rest[:].bitcast(I32), 0)
 
         z_k = keep.tile([P, PASSES, PACK, B], BF16)
         nc.sync.dma_start(
@@ -80,20 +76,29 @@ def tile_dynamix_pb_e_kernel(tc, z, mlp_out, t2, A, W_words, W_scales, h, out):
         nc.scalar.dma_start(out=logits[:], in_=mlp_out)
         t2_all = keep.tile([P, 1], BF16)
         nc.scalar.dma_start(out=t2_all[:], in_=t2.partition_broadcast(P))
-        load_scales(nc.sync, I32, planes_first, slice(0, first_passes), 2)
-        load_words(0, 2)
-        ah = keep.tile([P, 2, M], BF16)
-        nc.sync.dma_start(out=ah[:, 0, :], in_=A.unsqueeze(1).to_broadcast([E, COPIES, M]))
-        nc.sync.dma_start(out=ah[:, 1, :], in_=h.unsqueeze(1).to_broadcast([E, COPIES, M]))
-        load_words(2, E)
+        a_bf = keep.tile([E, M], BF16)
+        nc.scalar.dma_start(out=a_bf[:], in_=A)
+        h_bf = keep.tile([E, M], BF16)
+        nc.scalar.dma_start(out=h_bf[:], in_=h)
 
+        for group in range(GROUPS // 2):
+            zero_planes(group)
+        for group in range(GROUPS // 2):
+            load_scales(group)
+            load_words(group)
+
+        warm_in = keep.tile([P, 1], F32)
+        warm_out = keep.tile([P, 1], F32)
+        nc.gpsimd.memset(warm_in[:], 0.0)
+        nc.scalar.activation(out=warm_out[:], in_=warm_in[:], func=ACT.Exp)
         ident_f32 = keep.tile([P, P], F32)
         make_identity(nc, ident_f32[:])
+        ex_pad = keep.tile([P, P], F32)
+        nc.gpsimd.memset(ex_pad[:], 0.0)
+        ah32 = keep.tile([P, 2, M], F32)
+        nc.gpsimd.memset(ah32[:], 0.0)
         ident_bf = keep.tile([P, P], BF16)
         make_identity(nc, ident_bf[:])
-        ex_parts = keep.tile([P, E, COPIES], BF16)
-        nc.gpsimd.memset(ex_parts[:], 0.0)
-        load_scales(nc.gpsimd, F32, planes_rest, slice(first_passes, E * PASSES), 1)
 
         inv_t = keep.tile([P, 1], F32)
         nc.vector.reciprocal(out=inv_t[:], in_=t2_all[:])
@@ -101,9 +106,11 @@ def tile_dynamix_pb_e_kernel(tc, z, mlp_out, t2, A, W_words, W_scales, h, out):
         nc.vector.tensor_scalar(out=u[:], in0=logits[:], scalar1=inv_t[:], scalar2=None, op0=ALU.mult)
         u_min = keep.tile([P, 1], F32)
         nc.vector.tensor_reduce(out=u_min[:], in_=u[:], axis=AX.X, op=ALU.min)
-        ex = keep.tile([P, E], F32)
         ex_sum = keep.tile([P, 1], F32)
-        nc.scalar.activation(out=ex[:], in_=u[:], func=ACT.Exp, bias=u_min[:], scale=-1.0, accum_out=ex_sum[:])
+        nc.scalar.activation(
+            out=ex_pad[:, 0:E], in_=u[:], func=ACT.Exp, bias=u_min[:], scale=-1.0, accum_out=ex_sum[:]
+        )
+        nc.scalar.copy(out=ah32[0:E, 0, :], in_=a_bf[:])
 
         relu_parts = keep.tile([P, 1], F32)
         nc.vector.reduce_sum(out=relu_parts[:], in_=ident_f32[:, P - RELU_ROWS // PACK : P], axis=AX.X)
@@ -120,81 +127,72 @@ def tile_dynamix_pb_e_kernel(tc, z, mlp_out, t2, A, W_words, W_scales, h, out):
             )
         zq = keep.tile([P, PASSES * B], U32, align_bytes=64)
         zq_scales = keep.tile([P, PASSES * B], U8, align_bytes=64)
+        for group in range(GROUPS // 2, GROUPS):
+            zero_planes(group)
+        for group in range(GROUPS // 2, GROUPS):
+            load_scales(group)
+            load_words(group)
         inv_sum = keep.tile([P, 1], F32)
         nc.vector.reciprocal(out=inv_sum[:], in_=ex_sum[:])
         gate = keep.tile([P, E], F32)
-        nc.vector.tensor_scalar(out=gate[:], in0=ex[:], scalar1=inv_sum[:], scalar2=None, op0=ALU.mult)
+        nc.vector.tensor_scalar(out=gate[:], in0=ex_pad[:, 0:E], scalar1=inv_sum[:], scalar2=None, op0=ALU.mult)
         nc.vector.quantize_mx(
             out=zq[:].bitcast(FP8X4), scales=zq_scales[:], in_=grouped[:].rearrange("p g b j -> p (g b j)")
         )
-        left = ex
-        for part in range(PARTS):
-            nc.vector.tensor_copy(out=ex_parts[:, :, part], in_=left[:])
-            if part < PARTS - 1:
-                still_left = keep.tile([P, E], F32, name="left%d" % part)
-                nc.vector.tensor_tensor(out=still_left[:], in0=left[:], in1=ex_parts[:, :, part], op=ALU.subtract)
-                left = still_left
 
         zT_ps = psum.tile([P, PASSES, PACK, P], BF16, tag="bank")
         for g in range(PASSES):
             for j in range(PACK):
                 nc.tensor.transpose(out=zT_ps[:, g, j, :], in_=z_k[:, g, j, :], identity=ident_bf[:])
+        exT_ps = psum.tile([P, P], F32, tag="bank")
+        nc.tensor.transpose(out=exT_ps[:], in_=ex_pad[:], identity=ident_f32[:])
+        exT = keep.tile([P, P], F32)
+        nc.scalar.copy(out=exT[:], in_=exT_ps[:])
+        nc.scalar.copy(out=ah32[0:E, 1, :], in_=h_bf[:])
         zT = keep.tile([P, PASSES, P, PACK], BF16)
         nc.scalar.copy(out=zT[:], in_=zT_ps[:].rearrange("b g j p -> b g p j"))
-        exT_ps = psum.tile([P, P], BF16, tag="bank")
-        nc.tensor.transpose(out=exT_ps[:], in_=ex_parts[:].rearrange("b e i -> b (e i)"), identity=ident_bf[:])
-        exT = keep.tile([P, P], BF16)
-        nc.scalar.copy(out=exT[:], in_=exT_ps[:])
+        zT_m = zT[:].rearrange("b g p j -> b (g p j)")
 
         acc = keep.tile([P, M], F32)
-
-        def experts(first_expert, end_expert):
-            for e in range(first_expert, end_expert):
-                y = {}
-                for half in range(HALVES):
-                    y[half] = psum.tile([P, N_TILE], F32, tag="bank", name="y")
-                for c in range(PASSES):
-                    g = e * PASSES + c
-                    plane = planes_first[:, g, :] if e < FIRST_EXPERTS else planes_rest[:, g - first_passes, :]
-                    for half in range(HALVES):
-                        nc.tensor.matmul_mx(
-                            out=y[half][:],
-                            lhsT=zq[:, c * B : (c + 1) * B].bitcast(FP8X4),
-                            lhsT_scale=zq_scales[:, c * B : (c + 1) * B],
-                            rhs=words[:, g, half * 2 * N_TILE : (half + 1) * 2 * N_TILE].bitcast(FP4X4),
-                            rhs_scale=plane[:, half * N_TILE : (half + 1) * N_TILE],
-                            start=(c == 0),
-                            stop=(c == PASSES - 1),
-                        )
-                for half in range(HALVES):
-                    cols = slice(half * N_TILE, (half + 1) * N_TILE)
-                    if e == 0:
-                        nc.vector.tensor_scalar(
-                            out=acc[:, cols], in0=y[half][:], scalar1=gate[:, e : e + 1], scalar2=None, op0=ALU.mult
-                        )
-                    else:
-                        nc.vector.scalar_tensor_tensor(
-                            out=acc[:, cols], in0=y[half][:], scalar=gate[:, e : e + 1], in1=acc[:, cols],
-                            op0=ALU.mult, op1=ALU.add,
-                        )
-
-        experts(0, FIRST_EXPERTS)
-
-        gate_a = keep.tile([P, M], F32)
-        side = keep.tile([P, M], F32)
-        mixed_sb = (gate_a, side)
+        az = keep.tile([P, M], F32)
+        mixed = {}
         for term in range(2):
             for half in range(HALVES):
                 cols = slice(half * N_TILE, (half + 1) * N_TILE)
-                mixed = psum.tile([P, N_TILE], F32, tag="bank")
-                nc.tensor.matmul(out=mixed[:], lhsT=exT[:], rhs=ah[:, term, cols], start=True, stop=True)
-                nc.scalar.activation(out=mixed_sb[term][:, cols], in_=mixed[:], func=ACT.Copy, scale=inv_sum[:])
-        nc.gpsimd.tensor_tensor(out=gate_a[:], in0=gate_a[:], in1=zT[:].rearrange("b g p j -> b (g p j)"), op=ALU.mult)
-        nc.gpsimd.tensor_tensor(out=side[:], in0=side[:], in1=gate_a[:], op=ALU.add)
+                mixed[term, half] = psum.tile([P, N_TILE], F32, tag="bank", name="mixed")
+                nc.tensor.matmul(out=mixed[term, half][:], lhsT=exT[:], rhs=ah32[:, term, cols], start=True, stop=True)
+        for half in range(HALVES):
+            cols = slice(half * N_TILE, (half + 1) * N_TILE)
+            nc.vector.scalar_tensor_tensor(
+                out=az[:, cols], in0=mixed[0, half][:], scalar=inv_sum[:], in1=zT_m[:, cols], op0=ALU.mult, op1=ALU.mult
+            )
+        for half in range(HALVES):
+            cols = slice(half * N_TILE, (half + 1) * N_TILE)
+            nc.vector.scalar_tensor_tensor(
+                out=acc[:, cols], in0=mixed[1, half][:], scalar=inv_sum[:], in1=az[:, cols], op0=ALU.mult, op1=ALU.add
+            )
 
-        experts(FIRST_EXPERTS, E - LAST_EXPERTS)
-        nc.vector.tensor_tensor(out=acc[:], in0=acc[:], in1=side[:], op=ALU.add)
-        experts(E - LAST_EXPERTS, E)
+        for e in range(E):
+            y = {}
+            for half in range(HALVES):
+                y[half] = psum.tile([P, N_TILE], F32, tag="bank", name="y")
+            for c in range(PASSES):
+                g = e * PASSES + c
+                for half in range(HALVES):
+                    nc.tensor.matmul_mx(
+                        out=y[half][:],
+                        lhsT=zq[:, c * B : (c + 1) * B].bitcast(FP8X4),
+                        lhsT_scale=zq_scales[:, c * B : (c + 1) * B],
+                        rhs=words[:, g, half * 2 * N_TILE : (half + 1) * 2 * N_TILE].bitcast(FP4X4),
+                        rhs_scale=planes[e // GROUP_EXPERTS][:, g % GROUP_PASSES, half * N_TILE : (half + 1) * N_TILE],
+                        start=(c == 0),
+                        stop=(c == PASSES - 1),
+                    )
+            for half in range(HALVES):
+                cols = slice(half * N_TILE, (half + 1) * N_TILE)
+                nc.vector.scalar_tensor_tensor(
+                    out=acc[:, cols], in0=y[half][:], scalar=gate[:, e : e + 1], in1=acc[:, cols], op0=ALU.mult, op1=ALU.add
+                )
 
         out_pib = out.rearrange("(i p) b -> p i b", p=P)
         for half in range(HALVES):

@@ -27,10 +27,9 @@ HALVES = M // N_TILE
 M_TILES = N_TILE // P
 QUADRANT = 32
 
-GROUP_EXPERTS = 4
+GROUP_EXPERTS = 8
 GROUPS = E // GROUP_EXPERTS
 GROUP_PASSES = GROUP_EXPERTS * PASSES
-SCALE_DMA_PASSES = 4
 
 FLOPS = 2 * E * M * M * B
 
@@ -53,15 +52,13 @@ def tile_dynamix_pb_e_kernel(tc, z, mlp_out, t2, A, W_words, W_scales, h, out):
             nc.vector.memset(planes[group][:].bitcast(I32), 0)
 
         def load_scales(group):
-            for first in range(0, GROUP_PASSES, SCALE_DMA_PASSES):
-                local = slice(first, first + SCALE_DMA_PASSES)
-                passes = slice(group * GROUP_PASSES + first, group * GROUP_PASSES + first + SCALE_DMA_PASSES)
-                for s in range(2):
-                    for r in range(PACK):
-                        nc.sync.dma_start(
-                            out=planes[group][:].bitcast(I32)[QUADRANT * s + r : P : 2 * QUADRANT, local, :],
-                            in_=w_scales_i32[passes, PACK * s + r : 16 : 8, :].rearrange("g q n -> q g n"),
-                        )
+            passes = slice(group * GROUP_PASSES, (group + 1) * GROUP_PASSES)
+            for s in range(2):
+                for r in range(PACK):
+                    nc.sync.dma_start(
+                        out=planes[group][:].bitcast(I32)[QUADRANT * s + r : P : 2 * QUADRANT, :, :],
+                        in_=w_scales_i32[passes, PACK * s + r : 16 : 8, :].rearrange("g q n -> q g n"),
+                    )
 
         def load_words(group):
             for g in range(group * GROUP_PASSES, (group + 1) * GROUP_PASSES):

@@ -27,9 +27,10 @@ HALVES = M // N_TILE
 M_TILES = N_TILE // P
 QUADRANT = 32
 
-GROUP_EXPERTS = 8
+GROUP_EXPERTS = 4
 GROUPS = E // GROUP_EXPERTS
 GROUP_PASSES = GROUP_EXPERTS * PASSES
+SCALE_DMA_PASSES = 4
 
 FLOPS = 2 * E * M * M * B
 
@@ -52,12 +53,13 @@ def tile_dynamix_pb_e_kernel(tc, z, mlp_out, t2, A, W_words, W_scales, h, out):
             nc.vector.memset(planes[group][:].bitcast(I32), 0)
 
         def load_scales(group):
-            passes = slice(group * GROUP_PASSES, (group + 1) * GROUP_PASSES)
-            for s in range(2):
+            for first in range(0, GROUP_PASSES, SCALE_DMA_PASSES):
+                local = slice(first, first + SCALE_DMA_PASSES)
+                passes = slice(group * GROUP_PASSES + first, group * GROUP_PASSES + first + SCALE_DMA_PASSES)
                 for r in range(PACK):
                     nc.sync.dma_start(
-                        out=planes[group][:].bitcast(I32)[QUADRANT * s + r : P : 2 * QUADRANT, :, :],
-                        in_=w_scales_i32[passes, PACK * s + r : 16 : 8, :].rearrange("g q n -> q g n"),
+                        out=planes[group][:].bitcast(I32)[r : P : QUADRANT, local, :],
+                        in_=w_scales_i32[passes, r : 16 : PACK, :].rearrange("g q n -> q g n"),
                     )
 
         def load_words(group):

@@ -27,10 +27,10 @@ HALVES = M // N_TILE
 M_TILES = N_TILE // P
 QUADRANT = 32
 
-GROUP_EXPERTS = 4
+GROUP_EXPERTS = 2
 GROUPS = E // GROUP_EXPERTS
 GROUP_PASSES = GROUP_EXPERTS * PASSES
-SCALE_DMA_PASSES = 4
+RING = 4
 
 FLOPS = 2 * E * M * M * B
 
@@ -44,27 +44,29 @@ def tile_dynamix_pb_e_kernel(tc, z, mlp_out, t2, A, W_words, W_scales, h, out):
         ctx.enter_context(tc.manual_schedule())
 
         words = keep.tile([P, E * PASSES, 2 * M], U8, align_bytes=64)
-        planes = [keep.tile([P, GROUP_PASSES, M], U8, align_bytes=64, name="planes%d" % group) for group in range(GROUPS)]
+        planes = [keep.tile([P, GROUP_PASSES, M], U8, align_bytes=64, name="planes%d" % slot) for slot in range(RING)]
         words_i32 = words[:].bitcast(I32)
         w_words_i32 = W_words.bitcast(I32)
         w_scales_i32 = W_scales.bitcast(I32)
 
-        def zero_planes(group):
-            nc.vector.memset(planes[group][:].bitcast(I32), 0)
+        def zero_planes(slot):
+            nc.vector.memset(planes[slot][:].bitcast(I32), 0)
 
         def load_scales(group):
-            for first in range(0, GROUP_PASSES, SCALE_DMA_PASSES):
-                local = slice(first, first + SCALE_DMA_PASSES)
-                passes = slice(group * GROUP_PASSES + first, group * GROUP_PASSES + first + SCALE_DMA_PASSES)
-                for r in range(PACK):
-                    nc.sync.dma_start(
-                        out=planes[group][:].bitcast(I32)[r : P : QUADRANT, local, :],
-                        in_=w_scales_i32[passes, r : 16 : PACK, :].rearrange("g q n -> q g n"),
-                    )
+            passes = slice(group * GROUP_PASSES, (group + 1) * GROUP_PASSES)
+            for r in range(PACK):
+                nc.sync.dma_start(
+                    out=planes[group % RING][:].bitcast(I32)[r : P : QUADRANT, :, :],
+                    in_=w_scales_i32[passes, r : 16 : PACK, :].rearrange("g q n -> q g n"),
+                )
 
         def load_words(group):
-            for g in range(group * GROUP_PASSES, (group + 1) * GROUP_PASSES):
-                nc.sync.dma_start(out=words_i32[:, g, :], in_=w_words_i32[g])
+            for e in range(group * GROUP_EXPERTS, (group + 1) * GROUP_EXPERTS):
+                step = 1 if e == E - 1 else PASSES
+                for g in range(e * PASSES, (e + 1) * PASSES, step):
+                    nc.sync.dma_start(
+                        out=words_i32[:, g : g + step, :], in_=w_words_i32[g : g + step].rearrange("g p n -> p g n")
+                    )
 
         z_k = keep.tile([P, PASSES, PACK, B], BF16)
         nc.sync.dma_start(
@@ -80,9 +82,9 @@ def tile_dynamix_pb_e_kernel(tc, z, mlp_out, t2, A, W_words, W_scales, h, out):
         h_bf = keep.tile([E, M], BF16)
         nc.scalar.dma_start(out=h_bf[:], in_=h)
 
-        for group in range(GROUPS // 2):
-            zero_planes(group)
-        for group in range(GROUPS // 2):
+        for slot in range(RING):
+            zero_planes(slot)
+        for group in range(RING):
             load_scales(group)
             load_words(group)
 
@@ -126,11 +128,6 @@ def tile_dynamix_pb_e_kernel(tc, z, mlp_out, t2, A, W_words, W_scales, h, out):
             )
         zq = keep.tile([P, PASSES * B], U32, align_bytes=64)
         zq_scales = keep.tile([P, PASSES * B], U8, align_bytes=64)
-        for group in range(GROUPS // 2, GROUPS):
-            zero_planes(group)
-        for group in range(GROUPS // 2, GROUPS):
-            load_scales(group)
-            load_words(group)
         inv_sum = keep.tile([P, 1], F32)
         nc.vector.reciprocal(out=inv_sum[:], in_=ex_sum[:])
         gate = keep.tile([P, E], F32)
@@ -183,10 +180,13 @@ def tile_dynamix_pb_e_kernel(tc, z, mlp_out, t2, A, W_words, W_scales, h, out):
                         lhsT=zq[:, c * B : (c + 1) * B].bitcast(FP8X4),
                         lhsT_scale=zq_scales[:, c * B : (c + 1) * B],
                         rhs=words[:, g, half * 2 * N_TILE : (half + 1) * 2 * N_TILE].bitcast(FP4X4),
-                        rhs_scale=planes[e // GROUP_EXPERTS][:, g % GROUP_PASSES, half * N_TILE : (half + 1) * N_TILE],
+                        rhs_scale=planes[(e // GROUP_EXPERTS) % RING][:, g % GROUP_PASSES, half * N_TILE : (half + 1) * N_TILE],
                         start=(c == 0),
                         stop=(c == PASSES - 1),
                     )
+            if (e + 1) % GROUP_EXPERTS == 0 and e // GROUP_EXPERTS + RING < GROUPS:
+                load_scales(e // GROUP_EXPERTS + RING)
+                load_words(e // GROUP_EXPERTS + RING)
             for half in range(HALVES):
                 cols = slice(half * N_TILE, (half + 1) * N_TILE)
                 nc.vector.scalar_tensor_tensor(

@@ -24,13 +24,16 @@ RELU_ROWS = 32
 PASSES = M // K_PASS
 N_TILE = 512
 HALVES = M // N_TILE
-M_TILES = N_TILE // P
 QUADRANT = 32
 
 GROUP_EXPERTS = 2
 GROUPS = E // GROUP_EXPERTS
 GROUP_PASSES = GROUP_EXPERTS * PASSES
 RING = 4
+
+LOWEST = -3.4028234663852886e38
+SPLIT_ROWS = (4, 36, 68)
+SIDE_AFTER = 6
 
 FLOPS = 2 * E * M * M * B
 
@@ -39,7 +42,6 @@ def tile_dynamix_pb_e_kernel(tc, z, mlp_out, t2, A, W_words, W_scales, h, out):
     nc = tc.nc
     with ExitStack() as ctx:
         keep = ctx.enter_context(tc.tile_pool(name="keep", bufs=1))
-        stage = ctx.enter_context(tc.tile_pool(name="stage", bufs=2))
         psum = ctx.enter_context(tc.psum_pool(name="psum", bufs=8))
         ctx.enter_context(tc.manual_schedule())
 
@@ -52,15 +54,13 @@ def tile_dynamix_pb_e_kernel(tc, z, mlp_out, t2, A, W_words, W_scales, h, out):
         def zero_planes(slot):
             nc.vector.memset(planes[slot][:].bitcast(I32), 0)
 
-        def load_scales(group):
+        def load_group(group):
             passes = slice(group * GROUP_PASSES, (group + 1) * GROUP_PASSES)
             for r in range(PACK):
                 nc.sync.dma_start(
                     out=planes[group % RING][:].bitcast(I32)[r : P : QUADRANT, :, :],
                     in_=w_scales_i32[passes, r : 16 : PACK, :].rearrange("g q n -> q g n"),
                 )
-
-        def load_words(group):
             for e in range(group * GROUP_EXPERTS, (group + 1) * GROUP_EXPERTS):
                 step = 1 if e == E - 1 else PASSES
                 for g in range(e * PASSES, (e + 1) * PASSES, step):
@@ -70,36 +70,54 @@ def tile_dynamix_pb_e_kernel(tc, z, mlp_out, t2, A, W_words, W_scales, h, out):
 
         z_k = keep.tile([P, PASSES, PACK, B], BF16)
         nc.sync.dma_start(
-            out=z_k[:].rearrange("p g j b -> p g (j b)"),
-            in_=z.rearrange("(g p j) b -> p g (j b)", g=PASSES, p=P, j=PACK),
+            out=z_k[:].rearrange("p c j b -> p c (j b)"),
+            in_=z.rearrange("(c p j) b -> p c (j b)", c=PASSES, p=P, j=PACK),
         )
         logits = keep.tile([P, E], BF16)
         nc.scalar.dma_start(out=logits[:], in_=mlp_out)
         t2_all = keep.tile([P, 1], BF16)
         nc.scalar.dma_start(out=t2_all[:], in_=t2.partition_broadcast(P))
-        a_bf = keep.tile([E, M], BF16)
-        nc.scalar.dma_start(out=a_bf[:], in_=A)
-        h_bf = keep.tile([E, M], BF16)
-        nc.scalar.dma_start(out=h_bf[:], in_=h)
 
-        for slot in range(RING):
+        for slot in range(RING - 1):
             zero_planes(slot)
-        for group in range(RING):
-            load_scales(group)
-            load_words(group)
+        for group in range(RING - 1):
+            load_group(group)
 
         warm_in = keep.tile([P, 1], F32)
         warm_out = keep.tile([P, 1], F32)
         nc.gpsimd.memset(warm_in[:], 0.0)
         nc.scalar.activation(out=warm_out[:], in_=warm_in[:], func=ACT.Exp)
-        ident_f32 = keep.tile([P, P], F32)
-        make_identity(nc, ident_f32[:])
-        ex_pad = keep.tile([P, P], F32)
-        nc.gpsimd.memset(ex_pad[:], 0.0)
-        ah32 = keep.tile([P, 2, M], F32)
-        nc.gpsimd.memset(ah32[:], 0.0)
+        floor = keep.tile([P, 1], F32)
+        nc.gpsimd.memset(floor[:], LOWEST)
+        nc.gpsimd.affine_select(
+            out=floor[:],
+            in_=floor[:],
+            compare_op=ALU.is_ge,
+            fill=0.0,
+            base=P - RELU_ROWS // PACK - 1,
+            pattern=[[0, 1]],
+            channel_multiplier=-1,
+        )
+        gate_parts = keep.tile([P, P], BF16)
+        nc.gpsimd.memset(gate_parts[:], 0.0)
         ident_bf = keep.tile([P, P], BF16)
         make_identity(nc, ident_bf[:])
+
+        grouped = keep.tile([P, PASSES, B, PACK], BF16, align_bytes=64)
+        for c in range(PASSES):
+            z_bj = z_k[:, c].rearrange("p j b -> p b j")
+            if c < PASSES - 1:
+                nc.vector.tensor_copy(out=grouped[:, c], in_=z_bj)
+            else:
+                nc.vector.tensor_scalar(out=grouped[:, c], in0=z_bj, scalar1=floor[:], scalar2=None, op0=ALU.max)
+        zq = keep.tile([P, PASSES * B], U32, align_bytes=64)
+        zq_scales = keep.tile([P, PASSES * B], U8, align_bytes=64)
+        for c in range(PASSES):
+            nc.vector.quantize_mx(
+                out=zq[:, c * B : (c + 1) * B].bitcast(FP8X4),
+                scales=zq_scales[:, c * B : (c + 1) * B],
+                in_=grouped[:, c].rearrange("p b j -> p (b j)"),
+            )
 
         inv_t = keep.tile([P, 1], F32)
         nc.vector.reciprocal(out=inv_t[:], in_=t2_all[:])
@@ -107,67 +125,61 @@ def tile_dynamix_pb_e_kernel(tc, z, mlp_out, t2, A, W_words, W_scales, h, out):
         nc.vector.tensor_scalar(out=u[:], in0=logits[:], scalar1=inv_t[:], scalar2=None, op0=ALU.mult)
         u_min = keep.tile([P, 1], F32)
         nc.vector.tensor_reduce(out=u_min[:], in_=u[:], axis=AX.X, op=ALU.min)
+        ex = keep.tile([P, E], F32)
         ex_sum = keep.tile([P, 1], F32)
-        nc.scalar.activation(
-            out=ex_pad[:, 0:E], in_=u[:], func=ACT.Exp, bias=u_min[:], scale=-1.0, accum_out=ex_sum[:]
-        )
-        nc.scalar.copy(out=ah32[0:E, 0, :], in_=a_bf[:])
-
-        relu_parts = keep.tile([P, 1], F32)
-        nc.vector.reduce_sum(out=relu_parts[:], in_=ident_f32[:, P - RELU_ROWS // PACK : P], axis=AX.X)
-        rows_kept = keep.tile([P, PASSES], F32)
-        nc.vector.memset(rows_kept[:], 1.0)
-        nc.vector.tensor_scalar(
-            out=rows_kept[:, PASSES - 1 : PASSES], in0=relu_parts[:], scalar1=-1.0, scalar2=1.0, op0=ALU.mult, op1=ALU.add
-        )
-        grouped = keep.tile([P, PASSES, B, PACK], BF16, align_bytes=64)
-        for g in range(PASSES):
-            z_bj = z_k[:, g].rearrange("p j b -> p b j")
-            nc.vector.scalar_tensor_tensor(
-                out=grouped[:, g], in0=z_bj, scalar=rows_kept[:, g : g + 1], in1=z_bj, op0=ALU.mult, op1=ALU.max
-            )
-        zq = keep.tile([P, PASSES * B], U32, align_bytes=64)
-        zq_scales = keep.tile([P, PASSES * B], U8, align_bytes=64)
+        nc.scalar.activation(out=ex[:], in_=u[:], func=ACT.Exp, bias=u_min[:], scale=-1.0, accum_out=ex_sum[:])
         inv_sum = keep.tile([P, 1], F32)
         nc.vector.reciprocal(out=inv_sum[:], in_=ex_sum[:])
         gate = keep.tile([P, E], F32)
-        nc.vector.tensor_scalar(out=gate[:], in0=ex_pad[:, 0:E], scalar1=inv_sum[:], scalar2=None, op0=ALU.mult)
-        nc.vector.quantize_mx(
-            out=zq[:].bitcast(FP8X4), scales=zq_scales[:], in_=grouped[:].rearrange("p g b j -> p (g b j)")
-        )
+        nc.vector.tensor_scalar(out=gate[:], in0=ex[:], scalar1=inv_sum[:], scalar2=None, op0=ALU.mult)
+        zero_planes(RING - 1)
+        load_group(RING - 1)
 
-        zT_ps = psum.tile([P, PASSES, PACK, P], BF16, tag="bank")
-        for g in range(PASSES):
+        part = [gate_parts[:, row : row + E] for row in SPLIT_ROWS]
+        rest = keep.tile([P, E], F32)
+        nc.gpsimd.tensor_copy(out=part[0], in_=gate[:])
+        nc.gpsimd.tensor_tensor(out=rest[:], in0=gate[:], in1=part[0], op=ALU.subtract)
+        nc.gpsimd.tensor_copy(out=part[1], in_=rest[:])
+        nc.gpsimd.tensor_tensor(out=part[2], in0=rest[:], in1=part[1], op=ALU.subtract)
+        side_rows = {}
+        for name, source in (("a", A), ("h", h)):
+            side_rows[name] = keep.tile([P, M], BF16, name="rows_" + name)
+            nc.gpsimd.memset(side_rows[name][:].bitcast(F32), 0.0)
+        for name, source in (("a", A), ("h", h)):
+            for row in SPLIT_ROWS:
+                nc.gpsimd.dma_start(out=side_rows[name][row : row + E, :], in_=source)
+        ident_f32 = keep.tile([P, P], F32)
+        make_identity(nc, ident_f32[:])
+
+        gate_rows = keep.tile([P, B], BF16)
+
+        def transpose_gate():
+            gate_ps = psum.tile([P, B], BF16, tag="bank")
+            nc.tensor.transpose(out=gate_ps[:], in_=gate_parts[:], identity=ident_bf[:])
+            nc.scalar.copy(out=gate_rows[:], in_=gate_ps[:])
+
+        side = keep.tile([P, PASSES, PACK, B], F32)
+
+        def side_step(step):
+            c, name = step // 2, "ah"[step % 2]
+            mixed = psum.tile([P, PACK, B], F32, tag="bank")
             for j in range(PACK):
-                nc.tensor.transpose(out=zT_ps[:, g, j, :], in_=z_k[:, g, j, :], identity=ident_bf[:])
-        exT_ps = psum.tile([P, P], F32, tag="bank")
-        nc.tensor.transpose(out=exT_ps[:], in_=ex_pad[:], identity=ident_f32[:])
-        exT = keep.tile([P, P], F32)
-        nc.scalar.copy(out=exT[:], in_=exT_ps[:])
-        nc.scalar.copy(out=ah32[0:E, 1, :], in_=h_bf[:])
-        zT = keep.tile([P, PASSES, P, PACK], BF16)
-        nc.scalar.copy(out=zT[:], in_=zT_ps[:].rearrange("b g j p -> b g p j"))
-        zT_m = zT[:].rearrange("b g p j -> b (g p j)")
+                nc.tensor.matmul(
+                    out=mixed[:, j, :],
+                    lhsT=side_rows[name][:, c * K_PASS + j : (c + 1) * K_PASS : PACK],
+                    rhs=gate_rows[:],
+                    start=True,
+                    stop=True,
+                )
+            return c, name, mixed
+
+        def side_finish(c, name, mixed):
+            if name == "a":
+                nc.vector.tensor_tensor(out=side[:, c], in0=mixed[:], in1=z_k[:, c], op=ALU.mult)
+            else:
+                nc.vector.tensor_tensor(out=side[:, c], in0=mixed[:], in1=side[:, c], op=ALU.add)
 
         acc = keep.tile([P, M], F32)
-        az = keep.tile([P, M], F32)
-        mixed = {}
-        for term in range(2):
-            for half in range(HALVES):
-                cols = slice(half * N_TILE, (half + 1) * N_TILE)
-                mixed[term, half] = psum.tile([P, N_TILE], F32, tag="bank", name="mixed")
-                nc.tensor.matmul(out=mixed[term, half][:], lhsT=exT[:], rhs=ah32[:, term, cols], start=True, stop=True)
-        for half in range(HALVES):
-            cols = slice(half * N_TILE, (half + 1) * N_TILE)
-            nc.vector.scalar_tensor_tensor(
-                out=az[:, cols], in0=mixed[0, half][:], scalar=inv_sum[:], in1=zT_m[:, cols], op0=ALU.mult, op1=ALU.mult
-            )
-        for half in range(HALVES):
-            cols = slice(half * N_TILE, (half + 1) * N_TILE)
-            nc.vector.scalar_tensor_tensor(
-                out=acc[:, cols], in0=mixed[1, half][:], scalar=inv_sum[:], in1=az[:, cols], op0=ALU.mult, op1=ALU.add
-            )
-
         for e in range(E):
             y = {}
             for half in range(HALVES):
@@ -185,23 +197,28 @@ def tile_dynamix_pb_e_kernel(tc, z, mlp_out, t2, A, W_words, W_scales, h, out):
                         stop=(c == PASSES - 1),
                     )
             if (e + 1) % GROUP_EXPERTS == 0 and e // GROUP_EXPERTS + RING < GROUPS:
-                load_scales(e // GROUP_EXPERTS + RING)
-                load_words(e // GROUP_EXPERTS + RING)
+                load_group(e // GROUP_EXPERTS + RING)
+            if e == SIDE_AFTER - 3:
+                transpose_gate()
+            pending = side_step(e - SIDE_AFTER) if 0 <= e - SIDE_AFTER < 2 * PASSES else None
             for half in range(HALVES):
-                cols = slice(half * N_TILE, (half + 1) * N_TILE)
-                nc.vector.scalar_tensor_tensor(
-                    out=acc[:, cols], in0=y[half][:], scalar=gate[:, e : e + 1], in1=acc[:, cols], op0=ALU.mult, op1=ALU.add
-                )
+                y_jp = y[half][:].rearrange("b (p j) -> b j p", j=PACK)
+                acc_jp = acc[:, half * N_TILE : (half + 1) * N_TILE].rearrange("b (j p) -> b j p", j=PACK)
+                if e == 0:
+                    nc.vector.tensor_scalar(out=acc_jp, in0=y_jp, scalar1=gate[:, e : e + 1], scalar2=None, op0=ALU.mult)
+                else:
+                    nc.vector.scalar_tensor_tensor(
+                        out=acc_jp, in0=y_jp, scalar=gate[:, e : e + 1], in1=acc_jp, op0=ALU.mult, op1=ALU.add
+                    )
+            if pending is not None:
+                side_finish(*pending)
 
-        out_pib = out.rearrange("(i p) b -> p i b", p=P)
-        for half in range(HALVES):
-            accT = psum.tile([P, M_TILES, B], F32, tag="bank")
-            for i in range(M_TILES):
-                first = (half * M_TILES + i) * P
-                nc.tensor.transpose(out=accT[:, i, :], in_=acc[:, first : first + P], identity=ident_f32[:])
-            result = stage.tile([P, M_TILES, B], F32)
-            if half % 2 == 0:
-                nc.scalar.copy(out=result[:], in_=accT[:])
-            else:
-                nc.vector.tensor_copy(out=result[:], in_=accT[:])
-            nc.sync.dma_start(out=out_pib[:, half * M_TILES : (half + 1) * M_TILES, :], in_=result[:])
+        out_pcn = out.rearrange("(c p j) b -> p c (j b)", c=PASSES, p=P, j=PACK)
+        result = keep.tile([P, PASSES, PACK, B], F32)
+        for c in range(PASSES):
+            accT = psum.tile([P, PACK, B], F32, tag="bank")
+            for j in range(PACK):
+                first = (c * PACK + j) * P
+                nc.tensor.transpose(out=accT[:, j, :], in_=acc[:, first : first + P], identity=ident_f32[:])
+            nc.vector.tensor_tensor(out=result[:, c], in0=accT[:], in1=side[:, c], op=ALU.add)
+            nc.sync.dma_start(out=out_pcn[:, c, :], in_=result[:, c].rearrange("p j b -> p (j b)"))

@@ -26,10 +26,11 @@ N_TILE = 512
 HALVES = M // N_TILE
 QUADRANT = 32
 
-GROUP_EXPERTS = 2
+GROUP_EXPERTS = 4
 GROUPS = E // GROUP_EXPERTS
 GROUP_PASSES = GROUP_EXPERTS * PASSES
-RING = 4
+SCALE_DMA_PASSES = 4
+RING = 2
 
 LOWEST = -3.4028234663852886e38
 SPLIT_ROWS = (4, 36, 68)
@@ -54,19 +55,34 @@ def tile_dynamix_pb_e_kernel(tc, z, mlp_out, t2, A, W_words, W_scales, h, out):
         def zero_planes(slot):
             nc.vector.memset(planes[slot][:].bitcast(I32), 0)
 
-        def load_group(group):
-            passes = slice(group * GROUP_PASSES, (group + 1) * GROUP_PASSES)
-            for r in range(PACK):
-                nc.sync.dma_start(
-                    out=planes[group % RING][:].bitcast(I32)[r : P : QUADRANT, :, :],
-                    in_=w_scales_i32[passes, r : 16 : PACK, :].rearrange("g q n -> q g n"),
-                )
-            for e in range(group * GROUP_EXPERTS, (group + 1) * GROUP_EXPERTS):
-                step = 1 if e == E - 1 else PASSES
-                for g in range(e * PASSES, (e + 1) * PASSES, step):
+        def load_scales(group):
+            for first in range(0, GROUP_PASSES, SCALE_DMA_PASSES):
+                local = slice(first, first + SCALE_DMA_PASSES)
+                passes = slice(group * GROUP_PASSES + first, group * GROUP_PASSES + first + SCALE_DMA_PASSES)
+                for r in range(PACK):
                     nc.sync.dma_start(
-                        out=words_i32[:, g : g + step, :], in_=w_words_i32[g : g + step].rearrange("g p n -> p g n")
+                        out=planes[group % RING][:].bitcast(I32)[r : P : QUADRANT, local, :],
+                        in_=w_scales_i32[passes, r : 16 : PACK, :].rearrange("g q n -> q g n"),
                     )
+
+        def load_words(e):
+            first = e * PASSES
+            if e < E - 1:
+                for g in range(first, first + PASSES):
+                    nc.sync.dma_start(out=words_i32[:, g, :], in_=w_words_i32[g])
+            else:
+                split = N_TILE // 2
+                nc.sync.dma_start(
+                    out=words_i32[:, first : first + PASSES, 0:split],
+                    in_=w_words_i32[first : first + PASSES, :, 0:split].rearrange("g p n -> p g n"),
+                )
+                for g in range(first, first + PASSES):
+                    nc.sync.dma_start(out=words_i32[:, g, split : 2 * split], in_=w_words_i32[g, :, split : 2 * split])
+
+        def load_group(group, skip=0):
+            load_scales(group)
+            for e in range(group * GROUP_EXPERTS + skip, (group + 1) * GROUP_EXPERTS):
+                load_words(e)
 
         z_k = keep.tile([P, PASSES, PACK, B], BF16)
         nc.sync.dma_start(
@@ -78,10 +94,9 @@ def tile_dynamix_pb_e_kernel(tc, z, mlp_out, t2, A, W_words, W_scales, h, out):
         t2_all = keep.tile([P, 1], BF16)
         nc.scalar.dma_start(out=t2_all[:], in_=t2.partition_broadcast(P))
 
-        for slot in range(RING - 1):
-            zero_planes(slot)
-        for group in range(RING - 1):
-            load_group(group)
+        load_words(0)
+        zero_planes(0)
+        load_group(0, skip=1)
 
         warm_in = keep.tile([P, 1], F32)
         warm_out = keep.tile([P, 1], F32)
@@ -132,8 +147,8 @@ def tile_dynamix_pb_e_kernel(tc, z, mlp_out, t2, A, W_words, W_scales, h, out):
         nc.vector.reciprocal(out=inv_sum[:], in_=ex_sum[:])
         gate = keep.tile([P, E], F32)
         nc.vector.tensor_scalar(out=gate[:], in0=ex[:], scalar1=inv_sum[:], scalar2=None, op0=ALU.mult)
-        zero_planes(RING - 1)
-        load_group(RING - 1)
+        zero_planes(1)
+        load_group(1)
 
         part = [gate_parts[:, row : row + E] for row in SPLIT_ROWS]
         rest = keep.tile([P, E], F32)
@@ -184,18 +199,21 @@ def tile_dynamix_pb_e_kernel(tc, z, mlp_out, t2, A, W_words, W_scales, h, out):
             y = {}
             for half in range(HALVES):
                 y[half] = psum.tile([P, N_TILE], F32, tag="bank", name="y")
-            for c in range(PASSES):
+            if e < E - 1:
+                order = [(c, half) for c in range(PASSES) for half in range(HALVES)]
+            else:
+                order = [(c, half) for half in range(HALVES) for c in range(PASSES)]
+            for c, half in order:
                 g = e * PASSES + c
-                for half in range(HALVES):
-                    nc.tensor.matmul_mx(
-                        out=y[half][:],
-                        lhsT=zq[:, c * B : (c + 1) * B].bitcast(FP8X4),
-                        lhsT_scale=zq_scales[:, c * B : (c + 1) * B],
-                        rhs=words[:, g, half * 2 * N_TILE : (half + 1) * 2 * N_TILE].bitcast(FP4X4),
-                        rhs_scale=planes[(e // GROUP_EXPERTS) % RING][:, g % GROUP_PASSES, half * N_TILE : (half + 1) * N_TILE],
-                        start=(c == 0),
-                        stop=(c == PASSES - 1),
-                    )
+                nc.tensor.matmul_mx(
+                    out=y[half][:],
+                    lhsT=zq[:, c * B : (c + 1) * B].bitcast(FP8X4),
+                    lhsT_scale=zq_scales[:, c * B : (c + 1) * B],
+                    rhs=words[:, g, half * 2 * N_TILE : (half + 1) * 2 * N_TILE].bitcast(FP4X4),
+                    rhs_scale=planes[(e // GROUP_EXPERTS) % RING][:, g % GROUP_PASSES, half * N_TILE : (half + 1) * N_TILE],
+                    start=(c == 0),
+                    stop=(c == PASSES - 1),
+                )
             if (e + 1) % GROUP_EXPERTS == 0 and e // GROUP_EXPERTS + RING < GROUPS:
                 load_group(e // GROUP_EXPERTS + RING)
             if e == SIDE_AFTER - 3:
@@ -215,10 +233,12 @@ def tile_dynamix_pb_e_kernel(tc, z, mlp_out, t2, A, W_words, W_scales, h, out):
 
         out_pcn = out.rearrange("(c p j) b -> p c (j b)", c=PASSES, p=P, j=PACK)
         result = keep.tile([P, PASSES, PACK, B], F32)
+        acc_t = {}
         for c in range(PASSES):
-            accT = psum.tile([P, PACK, B], F32, tag="bank")
+            acc_t[c] = psum.tile([P, PACK, B], F32, tag="bank", name="acc_t")
             for j in range(PACK):
                 first = (c * PACK + j) * P
-                nc.tensor.transpose(out=accT[:, j, :], in_=acc[:, first : first + P], identity=ident_f32[:])
-            nc.vector.tensor_tensor(out=result[:, c], in0=accT[:], in1=side[:, c], op=ALU.add)
+                nc.tensor.transpose(out=acc_t[c][:, j, :], in_=acc[:, first : first + P], identity=ident_f32[:])
+        for c in range(PASSES):
+            nc.vector.tensor_tensor(out=result[:, c], in0=acc_t[c][:], in1=side[:, c], op=ALU.add)
             nc.sync.dma_start(out=out_pcn[:, c, :], in_=result[:, c].rearrange("p j b -> p (j b)"))

@@ -33,7 +33,8 @@ SCALE_DMA_PASSES = 4
 RING = 2
 
 LOWEST = -3.4028234663852886e38
-SPLIT_ROWS = (4, 36, 68)
+SPLIT_ROWS = (4, 5, 6)
+ROW_STEP = P // E
 SIDE_AFTER = 6
 
 FLOPS = 2 * E * M * M * B
@@ -150,7 +151,7 @@ def tile_dynamix_pb_e_kernel(tc, z, mlp_out, t2, A, W_words, W_scales, h, out):
         zero_planes(1)
         load_group(1)
 
-        part = [gate_parts[:, row : row + E] for row in SPLIT_ROWS]
+        part = [gate_parts[:, row : P : ROW_STEP] for row in SPLIT_ROWS]
         rest = keep.tile([P, E], F32)
         nc.gpsimd.tensor_copy(out=part[0], in_=gate[:])
         nc.gpsimd.tensor_tensor(out=rest[:], in0=gate[:], in1=part[0], op=ALU.subtract)
@@ -162,7 +163,7 @@ def tile_dynamix_pb_e_kernel(tc, z, mlp_out, t2, A, W_words, W_scales, h, out):
             nc.gpsimd.memset(side_rows[name][:].bitcast(F32), 0.0)
         for name, source in (("a", A), ("h", h)):
             for row in SPLIT_ROWS:
-                nc.gpsimd.dma_start(out=side_rows[name][row : row + E, :], in_=source)
+                nc.gpsimd.dma_start(out=side_rows[name][row : P : ROW_STEP, :], in_=source)
         ident_f32 = keep.tile([P, P], F32)
         make_identity(nc, ident_f32[:])
 

@@ -33,9 +33,10 @@ SCALE_DMA_PASSES = 4
 RING = 2
 
 LOWEST = -3.4028234663852886e38
-SPLIT_ROWS = (4, 5, 6)
+PARTS = 3
+FIRST_ROW = 4
 ROW_STEP = P // E
-SIDE_AFTER = 6
+SIDE_AFTER = {7: (0, 1), 11: (2, 3)}
 
 FLOPS = 2 * E * M * M * B
 
@@ -94,15 +95,20 @@ def tile_dynamix_pb_e_kernel(tc, z, mlp_out, t2, A, W_words, W_scales, h, out):
         nc.scalar.dma_start(out=logits[:], in_=mlp_out)
         t2_all = keep.tile([P, 1], BF16)
         nc.scalar.dma_start(out=t2_all[:], in_=t2.partition_broadcast(P))
+        warm_in = keep.tile([P, 1], F32)
+        warm_out = keep.tile([P, 1], F32)
+        nc.gpsimd.memset(warm_in[:], 0.0)
+        nc.scalar.activation(out=warm_out[:], in_=warm_in[:], func=ACT.Exp)
+        side_rows = {}
+        for name, source in (("a", A), ("h", h)):
+            side_rows[name] = keep.tile([P, M], BF16, name="rows_" + name)
+            nc.gpsimd.memset(side_rows[name][:].bitcast(F32), 0.0)
+            nc.scalar.dma_start(out=side_rows[name][FIRST_ROW : P : ROW_STEP, :], in_=source)
 
         load_words(0)
         zero_planes(0)
         load_group(0, skip=1)
 
-        warm_in = keep.tile([P, 1], F32)
-        warm_out = keep.tile([P, 1], F32)
-        nc.gpsimd.memset(warm_in[:], 0.0)
-        nc.scalar.activation(out=warm_out[:], in_=warm_in[:], func=ACT.Exp)
         floor = keep.tile([P, 1], F32)
         nc.gpsimd.memset(floor[:], LOWEST)
         nc.gpsimd.affine_select(
@@ -114,7 +120,7 @@ def tile_dynamix_pb_e_kernel(tc, z, mlp_out, t2, A, W_words, W_scales, h, out):
             pattern=[[0, 1]],
             channel_multiplier=-1,
         )
-        gate_parts = keep.tile([P, P], BF16)
+        gate_parts = keep.tile([P, PARTS, P], BF16)
         nc.gpsimd.memset(gate_parts[:], 0.0)
         ident_bf = keep.tile([P, P], BF16)
         make_identity(nc, ident_bf[:])
@@ -151,27 +157,21 @@ def tile_dynamix_pb_e_kernel(tc, z, mlp_out, t2, A, W_words, W_scales, h, out):
         zero_planes(1)
         load_group(1)
 
-        part = [gate_parts[:, row : P : ROW_STEP] for row in SPLIT_ROWS]
+        part = [gate_parts[:, k, FIRST_ROW : P : ROW_STEP] for k in range(PARTS)]
         rest = keep.tile([P, E], F32)
         nc.gpsimd.tensor_copy(out=part[0], in_=gate[:])
         nc.gpsimd.tensor_tensor(out=rest[:], in0=gate[:], in1=part[0], op=ALU.subtract)
         nc.gpsimd.tensor_copy(out=part[1], in_=rest[:])
         nc.gpsimd.tensor_tensor(out=part[2], in0=rest[:], in1=part[1], op=ALU.subtract)
-        side_rows = {}
-        for name, source in (("a", A), ("h", h)):
-            side_rows[name] = keep.tile([P, M], BF16, name="rows_" + name)
-            nc.gpsimd.memset(side_rows[name][:].bitcast(F32), 0.0)
-        for name, source in (("a", A), ("h", h)):
-            for row in SPLIT_ROWS:
-                nc.gpsimd.dma_start(out=side_rows[name][row : P : ROW_STEP, :], in_=source)
         ident_f32 = keep.tile([P, P], F32)
         make_identity(nc, ident_f32[:])
 
-        gate_rows = keep.tile([P, B], BF16)
+        gate_rows = keep.tile([P, PARTS, B], BF16)
 
         def transpose_gate():
-            gate_ps = psum.tile([P, B], BF16, tag="bank")
-            nc.tensor.transpose(out=gate_ps[:], in_=gate_parts[:], identity=ident_bf[:])
+            gate_ps = psum.tile([P, PARTS, B], BF16, tag="bank")
+            for k in range(PARTS):
+                nc.tensor.transpose(out=gate_ps[:, k, :], in_=gate_parts[:, k, :], identity=ident_bf[:])
             nc.scalar.copy(out=gate_rows[:], in_=gate_ps[:])
 
         side = keep.tile([P, PASSES, PACK, B], F32)
@@ -180,13 +180,14 @@ def tile_dynamix_pb_e_kernel(tc, z, mlp_out, t2, A, W_words, W_scales, h, out):
             c, name = step // 2, "ah"[step % 2]
             mixed = psum.tile([P, PACK, B], F32, tag="bank")
             for j in range(PACK):
-                nc.tensor.matmul(
-                    out=mixed[:, j, :],
-                    lhsT=side_rows[name][:, c * K_PASS + j : (c + 1) * K_PASS : PACK],
-                    rhs=gate_rows[:],
-                    start=True,
-                    stop=True,
-                )
+                for k in range(PARTS):
+                    nc.tensor.matmul(
+                        out=mixed[:, j, :],
+                        lhsT=side_rows[name][:, c * K_PASS + j : (c + 1) * K_PASS : PACK],
+                        rhs=gate_rows[:, k, :],
+                        start=(k == 0),
+                        stop=(k == PARTS - 1),
+                    )
             return c, name, mixed
 
         def side_finish(c, name, mixed):
@@ -217,9 +218,9 @@ def tile_dynamix_pb_e_kernel(tc, z, mlp_out, t2, A, W_words, W_scales, h, out):
                 )
             if (e + 1) % GROUP_EXPERTS == 0 and e // GROUP_EXPERTS + RING < GROUPS:
                 load_group(e // GROUP_EXPERTS + RING)
-            if e == SIDE_AFTER - 3:
+            if e == GROUP_EXPERTS - 1:
                 transpose_gate()
-            pending = side_step(e - SIDE_AFTER) if 0 <= e - SIDE_AFTER < 2 * PASSES else None
+            pending = [side_step(step) for step in SIDE_AFTER.get(e, ())]
             for half in range(HALVES):
                 y_jp = y[half][:].rearrange("b (p j) -> b j p", j=PACK)
                 acc_jp = acc[:, half * N_TILE : (half + 1) * N_TILE].rearrange("b (j p) -> b j p", j=PACK)
@@ -229,8 +230,8 @@ def tile_dynamix_pb_e_kernel(tc, z, mlp_out, t2, A, W_words, W_scales, h, out):
                     nc.vector.scalar_tensor_tensor(
                         out=acc_jp, in0=y_jp, scalar=gate[:, e : e + 1], in1=acc_jp, op0=ALU.mult, op1=ALU.add
                     )
-            if pending is not None:
-                side_finish(*pending)
+            for made in pending:
+                side_finish(*made)
 
         out_pcn = out.rearrange("(c p j) b -> p c (j b)", c=PASSES, p=P, j=PACK)
         result = keep.tile([P, PASSES, PACK, B], F32)

@@ -30,7 +30,6 @@ GROUP_EXPERTS = 4
 GROUPS = E // GROUP_EXPERTS
 GROUP_PASSES = GROUP_EXPERTS * PASSES
 SCALE_DMA_PASSES = 4
-RING = 2
 
 LOWEST = -3.4028234663852886e38
 PARTS = 3
@@ -49,42 +48,55 @@ def tile_dynamix_pb_e_kernel(tc, z, mlp_out, t2, A, W_words, W_scales, h, out):
         ctx.enter_context(tc.manual_schedule())
 
         words = keep.tile([P, E * PASSES, 2 * M], U8, align_bytes=64)
-        planes = [keep.tile([P, GROUP_PASSES, M], U8, align_bytes=64, name="planes%d" % slot) for slot in range(RING)]
+        planes = [keep.tile([P, GROUP_PASSES, M], U8, align_bytes=64, name="planes%d" % group) for group in range(GROUPS)]
         words_i32 = words[:].bitcast(I32)
         w_words_i32 = W_words.bitcast(I32)
         w_scales_i32 = W_scales.bitcast(I32)
 
-        def zero_planes(slot):
-            nc.vector.memset(planes[slot][:].bitcast(I32), 0)
+        def zero_planes(group):
+            nc.vector.memset(planes[group][:].bitcast(I32), 0)
 
-        def load_scales(group):
+        def scale_loads(group):
+            loads = []
             for first in range(0, GROUP_PASSES, SCALE_DMA_PASSES):
                 local = slice(first, first + SCALE_DMA_PASSES)
                 passes = slice(group * GROUP_PASSES + first, group * GROUP_PASSES + first + SCALE_DMA_PASSES)
                 for r in range(PACK):
-                    nc.sync.dma_start(
-                        out=planes[group % RING][:].bitcast(I32)[r : P : QUADRANT, local, :],
-                        in_=w_scales_i32[passes, r : 16 : PACK, :].rearrange("g q n -> q g n"),
+                    loads.append(
+                        (
+                            planes[group][:].bitcast(I32)[r : P : QUADRANT, local, :],
+                            w_scales_i32[passes, r : 16 : PACK, :].rearrange("g q n -> q g n"),
+                        )
                     )
+            return loads
 
-        def load_words(e):
+        def word_loads(e):
             first = e * PASSES
             if e < E - 1:
-                for g in range(first, first + PASSES):
-                    nc.sync.dma_start(out=words_i32[:, g, :], in_=w_words_i32[g])
-            else:
-                split = N_TILE // 2
-                nc.sync.dma_start(
-                    out=words_i32[:, first : first + PASSES, 0:split],
-                    in_=w_words_i32[first : first + PASSES, :, 0:split].rearrange("g p n -> p g n"),
+                return [(words_i32[:, g, :], w_words_i32[g]) for g in range(first, first + PASSES)]
+            split = N_TILE // 2
+            loads = [
+                (
+                    words_i32[:, first : first + PASSES, 0:split],
+                    w_words_i32[first : first + PASSES, :, 0:split].rearrange("g p n -> p g n"),
                 )
-                for g in range(first, first + PASSES):
-                    nc.sync.dma_start(out=words_i32[:, g, split : 2 * split], in_=w_words_i32[g, :, split : 2 * split])
+            ]
+            for g in range(first, first + PASSES):
+                loads.append((words_i32[:, g, split : 2 * split], w_words_i32[g, :, split : 2 * split]))
+            return loads
+
+        def issue(loads):
+            for target, source in loads:
+                nc.sync.dma_start(out=target, in_=source)
 
         def load_group(group, skip=0):
-            load_scales(group)
+            ahead = scale_loads(group + 1) if group + 1 < GROUPS else []
             for e in range(group * GROUP_EXPERTS + skip, (group + 1) * GROUP_EXPERTS):
-                load_words(e)
+                for load in word_loads(e):
+                    issue([load])
+                    issue(ahead[:1])
+                    ahead = ahead[1:]
+            issue(ahead)
 
         z_k = keep.tile([P, PASSES, PACK, B], BF16)
         nc.sync.dma_start(
@@ -105,8 +117,10 @@ def tile_dynamix_pb_e_kernel(tc, z, mlp_out, t2, A, W_words, W_scales, h, out):
             nc.gpsimd.memset(side_rows[name][:].bitcast(F32), 0.0)
             nc.scalar.dma_start(out=side_rows[name][FIRST_ROW : P : ROW_STEP, :], in_=source)
 
-        load_words(0)
+        issue(word_loads(0))
         zero_planes(0)
+        zero_planes(1)
+        issue(scale_loads(0))
         load_group(0, skip=1)
 
         floor = keep.tile([P, 1], F32)
@@ -154,8 +168,11 @@ def tile_dynamix_pb_e_kernel(tc, z, mlp_out, t2, A, W_words, W_scales, h, out):
         nc.vector.reciprocal(out=inv_sum[:], in_=ex_sum[:])
         gate = keep.tile([P, E], F32)
         nc.vector.tensor_scalar(out=gate[:], in0=ex[:], scalar1=inv_sum[:], scalar2=None, op0=ALU.mult)
-        zero_planes(1)
+        zero_planes(2)
         load_group(1)
+        zero_planes(3)
+        load_group(2)
+        load_group(3)
 
         part = [gate_parts[:, k, FIRST_ROW : P : ROW_STEP] for k in range(PARTS)]
         rest = keep.tile([P, E], F32)
@@ -212,12 +229,10 @@ def tile_dynamix_pb_e_kernel(tc, z, mlp_out, t2, A, W_words, W_scales, h, out):
                     lhsT=zq[:, c * B : (c + 1) * B].bitcast(FP8X4),
                     lhsT_scale=zq_scales[:, c * B : (c + 1) * B],
                     rhs=words[:, g, half * 2 * N_TILE : (half + 1) * 2 * N_TILE].bitcast(FP4X4),
-                    rhs_scale=planes[(e // GROUP_EXPERTS) % RING][:, g % GROUP_PASSES, half * N_TILE : (half + 1) * N_TILE],
+                    rhs_scale=planes[e // GROUP_EXPERTS][:, g % GROUP_PASSES, half * N_TILE : (half + 1) * N_TILE],
                     start=(c == 0),
                     stop=(c == PASSES - 1),
                 )
-            if (e + 1) % GROUP_EXPERTS == 0 and e // GROUP_EXPERTS + RING < GROUPS:
-                load_group(e // GROUP_EXPERTS + RING)
             if e == GROUP_EXPERTS - 1:
                 transpose_gate()
             pending = [side_step(step) for step in SIDE_AFTER.get(e, ())]

@@ -26,15 +26,16 @@ N_TILE = 512
 HALVES = M // N_TILE
 QUADRANT = 32
 
-GROUP_EXPERTS = 4
+GROUP_EXPERTS = 2
 GROUPS = E // GROUP_EXPERTS
 GROUP_PASSES = GROUP_EXPERTS * PASSES
-SCALE_DMA_PASSES = 4
+RING = 4
 
 LOWEST = -3.4028234663852886e38
 PARTS = 3
 FIRST_ROW = 4
 ROW_STEP = P // E
+GATE_AFTER = 3
 SIDE_AFTER = {7: (0, 1), 11: (2, 3)}
 
 FLOPS = 2 * E * M * M * B
@@ -48,27 +49,21 @@ def tile_dynamix_pb_e_kernel(tc, z, mlp_out, t2, A, W_words, W_scales, h, out):
         ctx.enter_context(tc.manual_schedule())
 
         words = keep.tile([P, E * PASSES, 2 * M], U8, align_bytes=64)
-        planes = [keep.tile([P, GROUP_PASSES, M], U8, align_bytes=64, name="planes%d" % group) for group in range(GROUPS)]
+        planes = [keep.tile([P, GROUP_PASSES, M], U8, align_bytes=64, name="planes%d" % slot) for slot in range(RING)]
         words_i32 = words[:].bitcast(I32)
         w_words_i32 = W_words.bitcast(I32)
         w_scales_i32 = W_scales.bitcast(I32)
 
-        def zero_planes(group):
-            nc.vector.memset(planes[group][:].bitcast(I32), 0)
+        def zero_planes(slot):
+            nc.vector.memset(planes[slot][:].bitcast(I32), 0)
 
         def scale_loads(group):
-            loads = []
-            for first in range(0, GROUP_PASSES, SCALE_DMA_PASSES):
-                local = slice(first, first + SCALE_DMA_PASSES)
-                passes = slice(group * GROUP_PASSES + first, group * GROUP_PASSES + first + SCALE_DMA_PASSES)
-                for r in range(PACK):
-                    loads.append(
-                        (
-                            planes[group][:].bitcast(I32)[r : P : QUADRANT, local, :],
-                            w_scales_i32[passes, r : 16 : PACK, :].rearrange("g q n -> q g n"),
-                        )
-                    )
-            return loads
+            passes = slice(group * GROUP_PASSES, (group + 1) * GROUP_PASSES)
+            target = planes[group % RING][:].bitcast(I32)
+            return [
+                (target[r : P : QUADRANT, :, :], w_scales_i32[passes, r : 16 : PACK, :].rearrange("g q n -> q g n"))
+                for r in range(PACK)
+            ]
 
         def word_loads(e):
             first = e * PASSES
@@ -89,39 +84,32 @@ def tile_dynamix_pb_e_kernel(tc, z, mlp_out, t2, A, W_words, W_scales, h, out):
             for target, source in loads:
                 nc.sync.dma_start(out=target, in_=source)
 
-        def load_group(group, skip=0):
+        def load_group(group):
             ahead = scale_loads(group + 1) if group + 1 < GROUPS else []
-            for e in range(group * GROUP_EXPERTS + skip, (group + 1) * GROUP_EXPERTS):
+            for e in range(group * GROUP_EXPERTS, (group + 1) * GROUP_EXPERTS):
                 for load in word_loads(e):
                     issue([load])
                     issue(ahead[:1])
                     ahead = ahead[1:]
-            issue(ahead)
 
         z_k = keep.tile([P, PASSES, PACK, B], BF16)
         nc.sync.dma_start(
             out=z_k[:].rearrange("p c j b -> p c (j b)"),
             in_=z.rearrange("(c p j) b -> p c (j b)", c=PASSES, p=P, j=PACK),
         )
+        for slot in range(RING):
+            zero_planes(slot)
         logits = keep.tile([P, E], BF16)
-        nc.scalar.dma_start(out=logits[:], in_=mlp_out)
+        nc.gpsimd.dma_start(out=logits[:], in_=mlp_out)
         t2_all = keep.tile([P, 1], BF16)
-        nc.scalar.dma_start(out=t2_all[:], in_=t2.partition_broadcast(P))
+        nc.gpsimd.dma_start(out=t2_all[:], in_=t2.partition_broadcast(P))
         warm_in = keep.tile([P, 1], F32)
         warm_out = keep.tile([P, 1], F32)
         nc.gpsimd.memset(warm_in[:], 0.0)
         nc.scalar.activation(out=warm_out[:], in_=warm_in[:], func=ACT.Exp)
-        side_rows = {}
-        for name, source in (("a", A), ("h", h)):
-            side_rows[name] = keep.tile([P, M], BF16, name="rows_" + name)
-            nc.gpsimd.memset(side_rows[name][:].bitcast(F32), 0.0)
-            nc.scalar.dma_start(out=side_rows[name][FIRST_ROW : P : ROW_STEP, :], in_=source)
-
-        issue(word_loads(0))
-        zero_planes(0)
-        zero_planes(1)
         issue(scale_loads(0))
-        load_group(0, skip=1)
+        for group in range(RING - 1):
+            load_group(group)
 
         floor = keep.tile([P, 1], F32)
         nc.gpsimd.memset(floor[:], LOWEST)
@@ -134,6 +122,11 @@ def tile_dynamix_pb_e_kernel(tc, z, mlp_out, t2, A, W_words, W_scales, h, out):
             pattern=[[0, 1]],
             channel_multiplier=-1,
         )
+        side_rows = {}
+        for name, source in (("a", A), ("h", h)):
+            side_rows[name] = keep.tile([P, M], BF16, name="rows_" + name)
+            nc.gpsimd.memset(side_rows[name][:].bitcast(F32), 0.0)
+            nc.gpsimd.dma_start(out=side_rows[name][FIRST_ROW : P : ROW_STEP, :], in_=source)
         gate_parts = keep.tile([P, PARTS, P], BF16)
         nc.gpsimd.memset(gate_parts[:], 0.0)
         ident_bf = keep.tile([P, P], BF16)
@@ -168,11 +161,6 @@ def tile_dynamix_pb_e_kernel(tc, z, mlp_out, t2, A, W_words, W_scales, h, out):
         nc.vector.reciprocal(out=inv_sum[:], in_=ex_sum[:])
         gate = keep.tile([P, E], F32)
         nc.vector.tensor_scalar(out=gate[:], in0=ex[:], scalar1=inv_sum[:], scalar2=None, op0=ALU.mult)
-        zero_planes(2)
-        load_group(1)
-        zero_planes(3)
-        load_group(2)
-        load_group(3)
 
         part = [gate_parts[:, k, FIRST_ROW : P : ROW_STEP] for k in range(PARTS)]
         rest = keep.tile([P, E], F32)
@@ -229,11 +217,13 @@ def tile_dynamix_pb_e_kernel(tc, z, mlp_out, t2, A, W_words, W_scales, h, out):
                     lhsT=zq[:, c * B : (c + 1) * B].bitcast(FP8X4),
                     lhsT_scale=zq_scales[:, c * B : (c + 1) * B],
                     rhs=words[:, g, half * 2 * N_TILE : (half + 1) * 2 * N_TILE].bitcast(FP4X4),
-                    rhs_scale=planes[e // GROUP_EXPERTS][:, g % GROUP_PASSES, half * N_TILE : (half + 1) * N_TILE],
+                    rhs_scale=planes[(e // GROUP_EXPERTS) % RING][:, g % GROUP_PASSES, half * N_TILE : (half + 1) * N_TILE],
                     start=(c == 0),
                     stop=(c == PASSES - 1),
                 )
-            if e == GROUP_EXPERTS - 1:
+            if (e + 1) % GROUP_EXPERTS == 0 and e // GROUP_EXPERTS + RING - 1 < GROUPS:
+                load_group(e // GROUP_EXPERTS + RING - 1)
+            if e == GATE_AFTER:
                 transpose_gate()
             pending = [side_step(step) for step in SIDE_AFTER.get(e, ())]
             for half in range(HALVES):

@@ -36,7 +36,7 @@ PARTS = 3
 FIRST_ROW = 4
 ROW_STEP = P // E
 GATE_AFTER = 3
-SIDE_AFTER = {7: (0, 1), 11: (2, 3)}
+SIDE_AFTER = {9: (0,), 10: (1,), 11: (2,), 12: (3,)}
 
 FLOPS = 2 * E * M * M * B
 
@@ -122,15 +122,18 @@ def tile_dynamix_pb_e_kernel(tc, z, mlp_out, t2, A, W_words, W_scales, h, out):
             pattern=[[0, 1]],
             channel_multiplier=-1,
         )
+        gate_parts = keep.tile([P, P], BF16)
+        nc.gpsimd.memset(gate_parts[:], 0.0)
+        ident_bf = keep.tile([P, P], BF16)
+        make_identity(nc, ident_bf[:])
+        ident_f32 = keep.tile([P, P], F32)
+        make_identity(nc, ident_f32[:])
         side_rows = {}
         for name, source in (("a", A), ("h", h)):
             side_rows[name] = keep.tile([P, M], BF16, name="rows_" + name)
             nc.gpsimd.memset(side_rows[name][:].bitcast(F32), 0.0)
-            nc.gpsimd.dma_start(out=side_rows[name][FIRST_ROW : P : ROW_STEP, :], in_=source)
-        gate_parts = keep.tile([P, PARTS, P], BF16)
-        nc.gpsimd.memset(gate_parts[:], 0.0)
-        ident_bf = keep.tile([P, P], BF16)
-        make_identity(nc, ident_bf[:])
+            for k in range(PARTS):
+                nc.gpsimd.dma_start(out=side_rows[name][FIRST_ROW + k : P : ROW_STEP, :], in_=source)
 
         grouped = keep.tile([P, PASSES, B, PACK], BF16, align_bytes=64)
         for c in range(PASSES):
@@ -162,44 +165,39 @@ def tile_dynamix_pb_e_kernel(tc, z, mlp_out, t2, A, W_words, W_scales, h, out):
         gate = keep.tile([P, E], F32)
         nc.vector.tensor_scalar(out=gate[:], in0=ex[:], scalar1=inv_sum[:], scalar2=None, op0=ALU.mult)
 
-        part = [gate_parts[:, k, FIRST_ROW : P : ROW_STEP] for k in range(PARTS)]
+        part = [gate_parts[:, FIRST_ROW + k : P : ROW_STEP] for k in range(PARTS)]
         rest = keep.tile([P, E], F32)
-        nc.gpsimd.tensor_copy(out=part[0], in_=gate[:])
-        nc.gpsimd.tensor_tensor(out=rest[:], in0=gate[:], in1=part[0], op=ALU.subtract)
-        nc.gpsimd.tensor_copy(out=part[1], in_=rest[:])
-        nc.gpsimd.tensor_tensor(out=part[2], in0=rest[:], in1=part[1], op=ALU.subtract)
-        ident_f32 = keep.tile([P, P], F32)
-        make_identity(nc, ident_f32[:])
+        nc.vector.tensor_copy(out=part[0], in_=gate[:])
+        nc.vector.tensor_tensor(out=rest[:], in0=gate[:], in1=part[0], op=ALU.subtract)
+        nc.vector.tensor_copy(out=part[1], in_=rest[:])
+        nc.vector.tensor_tensor(out=part[2], in0=rest[:], in1=part[1], op=ALU.subtract)
 
-        gate_rows = keep.tile([P, PARTS, B], BF16)
+        gate_rows = keep.tile([P, B], BF16)
 
         def transpose_gate():
-            gate_ps = psum.tile([P, PARTS, B], BF16, tag="bank")
-            for k in range(PARTS):
-                nc.tensor.transpose(out=gate_ps[:, k, :], in_=gate_parts[:, k, :], identity=ident_bf[:])
+            gate_ps = psum.tile([P, B], BF16, tag="bank")
+            nc.tensor.transpose(out=gate_ps[:], in_=gate_parts[:], identity=ident_bf[:])
             nc.scalar.copy(out=gate_rows[:], in_=gate_ps[:])
 
         side = keep.tile([P, PASSES, PACK, B], F32)
+        mixed = {name: keep.tile([P, PASSES, PACK, B], F32, name="mixed_" + name) for name in "ah"}
 
         def side_step(step):
             c, name = step // 2, "ah"[step % 2]
-            mixed = psum.tile([P, PACK, B], F32, tag="bank")
+            mixed_ps = psum.tile([P, PACK, B], F32, tag="bank")
             for j in range(PACK):
-                for k in range(PARTS):
-                    nc.tensor.matmul(
-                        out=mixed[:, j, :],
-                        lhsT=side_rows[name][:, c * K_PASS + j : (c + 1) * K_PASS : PACK],
-                        rhs=gate_rows[:, k, :],
-                        start=(k == 0),
-                        stop=(k == PARTS - 1),
-                    )
-            return c, name, mixed
-
-        def side_finish(c, name, mixed):
+                nc.tensor.matmul(
+                    out=mixed_ps[:, j, :],
+                    lhsT=side_rows[name][:, c * K_PASS + j : (c + 1) * K_PASS : PACK],
+                    rhs=gate_rows[:],
+                    start=True,
+                    stop=True,
+                )
+            nc.scalar.copy(out=mixed[name][:, c], in_=mixed_ps[:])
             if name == "a":
-                nc.vector.tensor_tensor(out=side[:, c], in0=mixed[:], in1=z_k[:, c], op=ALU.mult)
+                nc.gpsimd.tensor_tensor(out=side[:, c], in0=mixed[name][:, c], in1=z_k[:, c], op=ALU.mult)
             else:
-                nc.vector.tensor_tensor(out=side[:, c], in0=mixed[:], in1=side[:, c], op=ALU.add)
+                nc.gpsimd.tensor_tensor(out=side[:, c], in0=mixed[name][:, c], in1=side[:, c], op=ALU.add)
 
         acc = keep.tile([P, M], F32)
         for e in range(E):
@@ -225,7 +223,8 @@ def tile_dynamix_pb_e_kernel(tc, z, mlp_out, t2, A, W_words, W_scales, h, out):
                 load_group(e // GROUP_EXPERTS + RING - 1)
             if e == GATE_AFTER:
                 transpose_gate()
-            pending = [side_step(step) for step in SIDE_AFTER.get(e, ())]
+            for step in SIDE_AFTER.get(e, ()):
+                side_step(step)
             for half in range(HALVES):
                 y_jp = y[half][:].rearrange("b (p j) -> b j p", j=PACK)
                 acc_jp = acc[:, half * N_TILE : (half + 1) * N_TILE].rearrange("b (j p) -> b j p", j=PACK)
@@ -235,8 +234,6 @@ def tile_dynamix_pb_e_kernel(tc, z, mlp_out, t2, A, W_words, W_scales, h, out):
                     nc.vector.scalar_tensor_tensor(
                         out=acc_jp, in0=y_jp, scalar=gate[:, e : e + 1], in1=acc_jp, op0=ALU.mult, op1=ALU.add
                     )
-            for made in pending:
-                side_finish(*made)
 
         out_pcn = out.rearrange("(c p j) b -> p c (j b)", c=PASSES, p=P, j=PACK)
         result = keep.tile([P, PASSES, PACK, B], F32)

@@ -48,8 +48,8 @@ def tile_dynamix_pb_e_kernel(tc, z, mlp_out, t2, A, W_words, W_scales, h, out):
         psum = ctx.enter_context(tc.psum_pool(name="psum", bufs=8))
         ctx.enter_context(tc.manual_schedule())
 
-        words = keep.tile([P, E * PASSES, 2 * M], U8, align_bytes=64)
-        planes = [keep.tile([P, GROUP_PASSES, M], U8, align_bytes=64, name="planes%d" % slot) for slot in range(RING)]
+        words = keep.tile([P, E * PASSES, 2 * M], U8, align_bytes=256)
+        planes = [keep.tile([P, GROUP_PASSES, M], U8, align_bytes=256, name="planes%d" % slot) for slot in range(RING)]
         words_i32 = words[:].bitcast(I32)
         w_words_i32 = W_words.bitcast(I32)
         w_scales_i32 = W_scales.bitcast(I32)
@@ -92,7 +92,7 @@ def tile_dynamix_pb_e_kernel(tc, z, mlp_out, t2, A, W_words, W_scales, h, out):
                     issue(ahead[:1])
                     ahead = ahead[1:]
 
-        z_k = keep.tile([P, PASSES, PACK, B], BF16)
+        z_k = keep.tile([P, PASSES, PACK, B], BF16, align_bytes=256)
         nc.sync.dma_start(
             out=z_k[:].rearrange("p c j b -> p c (j b)"),
             in_=z.rearrange("(c p j) b -> p c (j b)", c=PASSES, p=P, j=PACK),
@@ -199,7 +199,13 @@ def tile_dynamix_pb_e_kernel(tc, z, mlp_out, t2, A, W_words, W_scales, h, out):
             else:
                 nc.gpsimd.tensor_tensor(out=side[:, c], in0=mixed[name][:, c], in1=side[:, c], op=ALU.add)
 
+        def turn(target, source, start, stop):
+            nc.tensor.matmul(out=target, lhsT=source, rhs=ident_f32[:], is_transpose=True, start=start, stop=stop)
+
         acc = keep.tile([P, M], F32)
+        last = keep.tile([P, PACK, P], F32)
+        middle = PACK // 2
+        acc_t = {}
         for e in range(E):
             y = {}
             for half in range(HALVES):
@@ -209,6 +215,10 @@ def tile_dynamix_pb_e_kernel(tc, z, mlp_out, t2, A, W_words, W_scales, h, out):
             else:
                 order = [(c, half) for half in range(HALVES) for c in range(PASSES)]
             for c, half in order:
+                if e == E - 1 and order.index((c, half)) == len(order) - 1:
+                    acc_t[0, 0] = psum.tile([P, PACK, B], F32, tag="bank", name="acc_t")
+                    for j in range(PACK):
+                        turn(acc_t[0, 0][:, j, :], acc[:, j * P : (j + 1) * P], start=(j == 0), stop=False)
                 g = e * PASSES + c
                 nc.tensor.matmul_mx(
                     out=y[half][:],
@@ -228,7 +238,9 @@ def tile_dynamix_pb_e_kernel(tc, z, mlp_out, t2, A, W_words, W_scales, h, out):
             for half in range(HALVES):
                 y_jp = y[half][:].rearrange("b (p j) -> b j p", j=PACK)
                 acc_jp = acc[:, half * N_TILE : (half + 1) * N_TILE].rearrange("b (j p) -> b j p", j=PACK)
-                if e == 0:
+                if e == E - 1 and half == 0:
+                    nc.scalar.activation(out=last[:], in_=y_jp, func=ACT.Copy, scale=gate[:, e : e + 1])
+                elif e == 0:
                     nc.vector.tensor_scalar(out=acc_jp, in0=y_jp, scalar1=gate[:, e : e + 1], scalar2=None, op0=ALU.mult)
                 else:
                     nc.vector.scalar_tensor_tensor(
@@ -236,13 +248,18 @@ def tile_dynamix_pb_e_kernel(tc, z, mlp_out, t2, A, W_words, W_scales, h, out):
                     )
 
         out_pcn = out.rearrange("(c p j) b -> p c (j b)", c=PASSES, p=P, j=PACK)
-        result = keep.tile([P, PASSES, PACK, B], F32)
-        acc_t = {}
-        for c in range(PASSES):
-            acc_t[c] = psum.tile([P, PACK, B], F32, tag="bank", name="acc_t")
-            for j in range(PACK):
-                first = (c * PACK + j) * P
-                nc.tensor.transpose(out=acc_t[c][:, j, :], in_=acc[:, first : first + P], identity=ident_f32[:])
-        for c in range(PASSES):
-            nc.vector.tensor_tensor(out=result[:, c], in0=acc_t[c][:], in1=side[:, c], op=ALU.add)
-            nc.sync.dma_start(out=out_pcn[:, c, :], in_=result[:, c].rearrange("p j b -> p (j b)"))
+        result = keep.tile([P, PASSES, PACK, B], F32, align_bytes=256)
+
+        def finish(c, j0, j1):
+            nc.vector.tensor_tensor(out=result[:, c, j0:j1, :], in0=acc_t[c, j0][:], in1=side[:, c, j0:j1, :], op=ALU.add)
+            nc.sync.dma_start(out=out_pcn[:, c, j0 * B : j1 * B], in_=result[:, c, j0:j1, :].rearrange("p j b -> p (j b)"))
+
+        for j in range(PACK):
+            turn(acc_t[0, 0][:, j, :], last[:, j, :], start=False, stop=(j == PACK - 1))
+        for j0 in (0, middle):
+            acc_t[1, j0] = psum.tile([P, middle, B], F32, tag="bank", name="acc_t")
+            for j in range(j0, j0 + middle):
+                turn(acc_t[1, j0][:, j - j0, :], acc[:, N_TILE + j * P : N_TILE + (j + 1) * P], start=True, stop=True)
+        finish(0, 0, PACK)
+        finish(1, 0, middle)
+        finish(1, middle, PACK)

@@ -252,7 +252,9 @@ def tile_dynamix_pb_e_kernel(tc, z, mlp_out, t2, A, W_words, W_scales, h, out):
 
         def finish(c, j0, j1):
             nc.vector.tensor_tensor(out=result[:, c, j0:j1, :], in0=acc_t[c, j0][:], in1=side[:, c, j0:j1, :], op=ALU.add)
-            nc.sync.dma_start(out=out_pcn[:, c, j0 * B : j1 * B], in_=result[:, c, j0:j1, :].rearrange("p j b -> p (j b)"))
+
+        def store(c):
+            nc.sync.dma_start(out=out_pcn[:, c, :], in_=result[:, c].rearrange("p j b -> p (j b)"))
 
         for j in range(PACK):
             turn(acc_t[0, 0][:, j, :], last[:, j, :], start=False, stop=(j == PACK - 1))
@@ -261,5 +263,7 @@ def tile_dynamix_pb_e_kernel(tc, z, mlp_out, t2, A, W_words, W_scales, h, out):
             for j in range(j0, j0 + middle):
                 turn(acc_t[1, j0][:, j - j0, :], acc[:, N_TILE + j * P : N_TILE + (j + 1) * P], start=True, stop=True)
         finish(0, 0, PACK)
+        store(0)
         finish(1, 0, middle)
         finish(1, middle, PACK)
+        store(1)

from contextlib import ExitStack

import concourse.mybir as mybir
from concourse.masks import make_identity

F32 = mybir.dt.float32
BF16 = mybir.dt.bfloat16
I32 = mybir.dt.int32
U32 = mybir.dt.uint32
U8 = mybir.dt.uint8
FP8X4 = mybir.dt.float8_e4m3fn_x4
FP4X4 = mybir.dt.float4_e2m1fn_x4
ALU = mybir.AluOpType
ACT = mybir.ActivationFunctionType
AX = mybir.AxisListType

P = 128
PACK = 4
K_PASS = P * PACK
M = 1024
B = 128
E = 16
RELU_ROWS = 32
PASSES = M // K_PASS
N_TILE = 512
HALVES = M // N_TILE
QUADRANT = 32

GROUP_EXPERTS = 2
GROUPS = E // GROUP_EXPERTS
GROUP_PASSES = GROUP_EXPERTS * PASSES
RING = 4

LOWEST = -3.4028234663852886e38
PARTS = 3
FIRST_ROW = 4
ROW_STEP = P // E
GATE_AFTER = 3
SIDE_AFTER = {9: (0,), 10: (1,), 11: (2,), 12: (3,)}

FLOPS = 2 * E * M * M * B


def tile_dynamix_pb_e_kernel(tc, z, mlp_out, t2, A, W_words, W_scales, h, out):
    nc = tc.nc
    with ExitStack() as ctx:
        keep = ctx.enter_context(tc.tile_pool(name="keep", bufs=1))
        psum = ctx.enter_context(tc.psum_pool(name="psum", bufs=8))
        ctx.enter_context(tc.manual_schedule())

        words = keep.tile([P, E * PASSES, 2 * M], U8, align_bytes=256)
        planes = [keep.tile([P, GROUP_PASSES, M], U8, align_bytes=256, name="planes%d" % slot) for slot in range(RING)]
        words_i32 = words[:].bitcast(I32)
        w_words_i32 = W_words.bitcast(I32)
        w_scales_i32 = W_scales.bitcast(I32)

        def zero_planes(slot):
            nc.vector.memset(planes[slot][:].bitcast(I32), 0)

        def scale_loads(group):
            passes = slice(group * GROUP_PASSES, (group + 1) * GROUP_PASSES)
            target = planes[group % RING][:].bitcast(I32)
            return [
                (target[r : P : QUADRANT, :, :], w_scales_i32[passes, r : 16 : PACK, :].rearrange("g q n -> q g n"))
                for r in range(PACK)
            ]

        def word_loads(e):
            first = e * PASSES
            if e < E - 1:
                return [(words_i32[:, g, :], w_words_i32[g]) for g in range(first, first + PASSES)]
            split = N_TILE // 2
            loads = [
                (
                    words_i32[:, first : first + PASSES, 0:split],
                    w_words_i32[first : first + PASSES, :, 0:split].rearrange("g p n -> p g n"),
                )
            ]
            for g in range(first, first + PASSES):
                loads.append((words_i32[:, g, split : 2 * split], w_words_i32[g, :, split : 2 * split]))
            return loads

        def issue(loads):
            for target, source in loads:
                nc.sync.dma_start(out=target, in_=source)

        def load_group(group):
            ahead = scale_loads(group + 1) if group + 1 < GROUPS else []
            for e in range(group * GROUP_EXPERTS, (group + 1) * GROUP_EXPERTS):
                for load in word_loads(e):
                    issue([load])
                    issue(ahead[:1])
                    ahead = ahead[1:]

        z_k = keep.tile([P, PASSES, PACK, B], BF16, align_bytes=256)
        nc.sync.dma_start(
            out=z_k[:].rearrange("p c j b -> p c (j b)"),
            in_=z.rearrange("(c p j) b -> p c (j b)", c=PASSES, p=P, j=PACK),
        )
        for slot in range(RING):
            zero_planes(slot)
        logits = keep.tile([P, E], BF16)
        nc.gpsimd.dma_start(out=logits[:], in_=mlp_out)
        t2_all = keep.tile([P, 1], BF16)
        nc.gpsimd.dma_start(out=t2_all[:], in_=t2.partition_broadcast(P))
        warm_in = keep.tile([P, 1], F32)
        warm_out = keep.tile([P, 1], F32)
        nc.gpsimd.memset(warm_in[:], 0.0)
        nc.scalar.activation(out=warm_out[:], in_=warm_in[:], func=ACT.Exp)
        issue(scale_loads(0))
        for group in range(RING - 1):
            load_group(group)

        floor = keep.tile([P, 1], F32)
        nc.gpsimd.memset(floor[:], LOWEST)
        nc.gpsimd.affine_select(
            out=floor[:],
            in_=floor[:],
            compare_op=ALU.is_ge,
            fill=0.0,
            base=P - RELU_ROWS // PACK - 1,
            pattern=[[0, 1]],
            channel_multiplier=-1,
        )
        gate_parts = keep.tile([P, P], BF16)
        nc.gpsimd.memset(gate_parts[:], 0.0)
        ident_bf = keep.tile([P, P], BF16)
        make_identity(nc, ident_bf[:])
        ident_f32 = keep.tile([P, P], F32)
        make_identity(nc, ident_f32[:])
        side_rows = {}
        for name, source in (("a", A), ("h", h)):
            side_rows[name] = keep.tile([P, M], BF16, name="rows_" + name)
            nc.gpsimd.memset(side_rows[name][:].bitcast(F32), 0.0)
            for k in range(PARTS):
                nc.gpsimd.dma_start(out=side_rows[name][FIRST_ROW + k : P : ROW_STEP, :], in_=source)

        grouped = keep.tile([P, PASSES, B, PACK], BF16, align_bytes=64)
        for c in range(PASSES):
            z_bj = z_k[:, c].rearrange("p j b -> p b j")
            if c < PASSES - 1:
                nc.vector.tensor_copy(out=grouped[:, c], in_=z_bj)
            else:
                nc.vector.tensor_scalar(out=grouped[:, c], in0=z_bj, scalar1=floor[:], scalar2=None, op0=ALU.max)
        zq = keep.tile([P, PASSES * B], U32, align_bytes=64)
        zq_scales = keep.tile([P, PASSES * B], U8, align_bytes=64)
        for c in range(PASSES):
            nc.vector.quantize_mx(
                out=zq[:, c * B : (c + 1) * B].bitcast(FP8X4),
                scales=zq_scales[:, c * B : (c + 1) * B],
                in_=grouped[:, c].rearrange("p b j -> p (b j)"),
            )

        inv_t = keep.tile([P, 1], F32)
        nc.vector.reciprocal(out=inv_t[:], in_=t2_all[:])
        u = keep.tile([P, E], F32)
        nc.vector.tensor_scalar(out=u[:], in0=logits[:], scalar1=inv_t[:], scalar2=None, op0=ALU.mult)
        u_min = keep.tile([P, 1], F32)
        nc.vector.tensor_reduce(out=u_min[:], in_=u[:], axis=AX.X, op=ALU.min)
        ex = keep.tile([P, E], F32)
        ex_sum = keep.tile([P, 1], F32)
        nc.scalar.activation(out=ex[:], in_=u[:], func=ACT.Exp, bias=u_min[:], scale=-1.0, accum_out=ex_sum[:])
        inv_sum = keep.tile([P, 1], F32)
        nc.vector.reciprocal(out=inv_sum[:], in_=ex_sum[:])
        gate = keep.tile([P, E], F32)
        nc.vector.tensor_scalar(out=gate[:], in0=ex[:], scalar1=inv_sum[:], scalar2=None, op0=ALU.mult)

        part = [gate_parts[:, FIRST_ROW + k : P : ROW_STEP] for k in range(PARTS)]
        rest = keep.tile([P, E], F32)
        nc.vector.tensor_copy(out=part[0], in_=gate[:])
        nc.vector.tensor_tensor(out=rest[:], in0=gate[:], in1=part[0], op=ALU.subtract)
        nc.vector.tensor_copy(out=part[1], in_=rest[:])
        nc.vector.tensor_tensor(out=part[2], in0=rest[:], in1=part[1], op=ALU.subtract)

        gate_rows = keep.tile([P, B], BF16)

        def transpose_gate():
            gate_ps = psum.tile([P, B], BF16, tag="bank")
            nc.tensor.transpose(out=gate_ps[:], in_=gate_parts[:], identity=ident_bf[:])
            nc.scalar.copy(out=gate_rows[:], in_=gate_ps[:])

        side = keep.tile([P, PASSES, PACK, B], F32)
        mixed = {name: keep.tile([P, PASSES, PACK, B], F32, name="mixed_" + name) for name in "ah"}

        def side_step(step):
            c, name = step // 2, "ah"[step % 2]
            mixed_ps = psum.tile([P, PACK, B], F32, tag="bank")
            for j in range(PACK):
                nc.tensor.matmul(
                    out=mixed_ps[:, j, :],
                    lhsT=side_rows[name][:, c * K_PASS + j : (c + 1) * K_PASS : PACK],
                    rhs=gate_rows[:],
                    start=True,
                    stop=True,
                )
            nc.scalar.copy(out=mixed[name][:, c], in_=mixed_ps[:])
            if name == "a":
                nc.gpsimd.tensor_tensor(out=side[:, c], in0=mixed[name][:, c], in1=z_k[:, c], op=ALU.mult)
            else:
                nc.gpsimd.tensor_tensor(out=side[:, c], in0=mixed[name][:, c], in1=side[:, c], op=ALU.add)

        def turn(target, source, start, stop):
            nc.tensor.matmul(out=target, lhsT=source, rhs=ident_f32[:], is_transpose=True, start=start, stop=stop)

        acc = keep.tile([P, M], F32)
        last = keep.tile([P, PACK, P], F32)
        middle = PACK // 2
        acc_t = {}
        for e in range(E):
            y = {}
            for half in range(HALVES):
                y[half] = psum.tile([P, N_TILE], F32, tag="bank", name="y")
            if e < E - 1:
                order = [(c, half) for c in range(PASSES) for half in range(HALVES)]
            else:
                order = [(c, half) for half in range(HALVES) for c in range(PASSES)]
            for c, half in order:
                if e == E - 1 and order.index((c, half)) == len(order) - 1:
                    acc_t[0, 0] = psum.tile([P, PACK, B], F32, tag="bank", name="acc_t")
                    for j in range(PACK):
                        turn(acc_t[0, 0][:, j, :], acc[:, j * P : (j + 1) * P], start=(j == 0), stop=False)
                g = e * PASSES + c
                nc.tensor.matmul_mx(
                    out=y[half][:],
                    lhsT=zq[:, c * B : (c + 1) * B].bitcast(FP8X4),
                    lhsT_scale=zq_scales[:, c * B : (c + 1) * B],
                    rhs=words[:, g, half * 2 * N_TILE : (half + 1) * 2 * N_TILE].bitcast(FP4X4),
                    rhs_scale=planes[(e // GROUP_EXPERTS) % RING][:, g % GROUP_PASSES, half * N_TILE : (half + 1) * N_TILE],
                    start=(c == 0),
                    stop=(c == PASSES - 1),
                )
            if (e + 1) % GROUP_EXPERTS == 0 and e // GROUP_EXPERTS + RING - 1 < GROUPS:
                load_group(e // GROUP_EXPERTS + RING - 1)
            if e == GATE_AFTER:
                transpose_gate()
            for step in SIDE_AFTER.get(e, ()):
                side_step(step)
            for half in range(HALVES):
                y_jp = y[half][:].rearrange("b (p j) -> b j p", j=PACK)
                acc_jp = acc[:, half * N_TILE : (half + 1) * N_TILE].rearrange("b (j p) -> b j p", j=PACK)
                if e == E - 1 and half == 0:
                    nc.scalar.activation(out=last[:], in_=y_jp, func=ACT.Copy, scale=gate[:, e : e + 1])
                elif e == 0:
                    nc.vector.tensor_scalar(out=acc_jp, in0=y_jp, scalar1=gate[:, e : e + 1], scalar2=None, op0=ALU.mult)
                else:
                    nc.vector.scalar_tensor_tensor(
                        out=acc_jp, in0=y_jp, scalar=gate[:, e : e + 1], in1=acc_jp, op0=ALU.mult, op1=ALU.add
                    )

        out_pcn = out.rearrange("(c p j) b -> p c (j b)", c=PASSES, p=P, j=PACK)
        result = keep.tile([P, PASSES, PACK, B], F32, align_bytes=256)

        def finish(c, j0, j1):
            nc.vector.tensor_tensor(out=result[:, c, j0:j1, :], in0=acc_t[c, j0][:], in1=side[:, c, j0:j1, :], op=ALU.add)

        def store(c):
            nc.sync.dma_start(out=out_pcn[:, c, :], in_=result[:, c].rearrange("p j b -> p (j b)"))

        for j in range(PACK):
            turn(acc_t[0, 0][:, j, :], last[:, j, :], start=False, stop=(j == PACK - 1))
        for j0 in (0, middle):
            acc_t[1, j0] = psum.tile([P, middle, B], F32, tag="bank", name="acc_t")
            for j in range(j0, j0 + middle):
                turn(acc_t[1, j0][:, j - j0, :], acc[:, N_TILE + j * P : N_TILE + (j + 1) * P], start=True, stop=True)
        finish(0, 0, PACK)
        store(0)
        finish(1, 0, middle)
        finish(1, middle, PACK)
        store(1)
